import numpy as np
import ml_dtypes


def mxq(x, axis, fmt="e4m3"):
    dtype, down = {"e4m3": (ml_dtypes.float8_e4m3fn, 7), "e5m2": (ml_dtypes.float8_e5m2, 14)}[fmt]
    v = np.moveaxis(np.asarray(x, np.float32).astype(ml_dtypes.bfloat16).astype(np.float64), axis, -1)
    blocks = v.reshape(v.shape[:-1] + (-1, 32))
    amax = np.abs(blocks).max(-1, keepdims=True)
    byte = np.maximum(np.where(amax > 0, np.frexp(amax)[1] - 1 + 127, 0) - down, 1)
    scale = np.exp2(byte - 127.0)
    codes = (blocks / scale).astype(np.float32).astype(dtype).astype(np.float64)
    return np.moveaxis((codes * scale).reshape(v.shape), -1, axis)


WIDE = False


def mx_kscale(k):
    if not WIDE:
        return np.ones(k)
    levels = np.array([10, -10, 5, -5, 0])
    a = np.random.permutation(np.resize(levels, k // 512 * 4)).reshape(k // 512, 4)
    idx = np.arange(k)
    return np.exp2(a[idx // 512, idx % 128 // 32])


BF16 = ml_dtypes.bfloat16


def bf(x):
    return np.asarray(x, np.float32).astype(BF16)


def f64(x):
    return np.asarray(x).astype(np.float64)


B, I, J, P = 1024, 512, 512, 8
TEMP = 1.0


def primitives(x):
    return np.stack([np.zeros_like(x), x, x * x, x * x * x, np.exp(x), np.log(x), 1.0 / x, np.sin(x)], axis=-1)


def setup_inputs():
    r = np.exp2(np.round(np.log2(mx_kscale(I)) / 3))
    g = np.exp2(np.round(1.5 * (r - 1.0) / np.log(2.0)))
    one = np.ones(I)
    undo = np.stack([one, 1.0 / r, 1.0 / r**2, 1.0 / r**3, 1.0 / g, one, r, one], axis=-1)
    return {"x": bf((np.random.random_sample((B, I)) + 0.5) * r),
            "alphas": bf(np.random.standard_normal((I, J, P))),
            "coeffs": bf(np.random.standard_normal((I, J, P)) * 3.0 / np.sqrt(I) * undo[:, None, :])}


def reference(x, alphas, coeffs):
    a = f64(alphas) / TEMP
    e = np.exp(a - a.max(-1, keepdims=True))
    gates = e / e.sum(-1, keepdims=True)
    prims = primitives(f64(x))
    w = gates * f64(coeffs)
    p = prims[:, :, 1:].transpose(2, 0, 1)
    v = w[:, :, 1:].transpose(2, 0, 1)
    return (mxq(p, 2, "e4m3") @ mxq(v, 1, "e4m3")).sum(0)

@@ -1,0 +1,237 @@
+import math
+from contextlib import ExitStack
+
+import concourse.mybir as mybir
+from concourse.masks import make_identity
+
+F32 = mybir.dt.float32
+BF16 = mybir.dt.bfloat16
+I32 = mybir.dt.int32
+U32 = mybir.dt.uint32
+U8 = mybir.dt.uint8
+FP8X4 = mybir.dt.float8_e4m3fn_x4
+ALU = mybir.AluOpType
+ACT = mybir.ActivationFunctionType
+
+P = 128
+B, I, J, K = 1024, 512, 512, 8
+NB = B // P
+PACK = 4
+JC = 128
+NCH = J // JC
+NPRIM = K - 1
+XW = NB * P * PACK
+CW = JC * PACK
+
+FLOPS = 2 * B * I * J * NPRIM
+
+
+def tile_dartslayer_kernel(tc, x, alphas, coeffs, out):
+    nc = tc.nc
+    with ExitStack() as ctx:
+        const = ctx.enter_context(tc.tile_pool(name="const", bufs=1))
+        big = ctx.enter_context(tc.tile_pool(name="big", bufs=5))
+        acp = ctx.enter_context(tc.tile_pool(name="acp", bufs=5))
+        k8 = ctx.enter_context(tc.tile_pool(name="k8", bufs=4))
+        keep = ctx.enter_context(tc.tile_pool(name="keep", bufs=1))
+        mt = ctx.enter_context(tc.tile_pool(name="mt", bufs=1))
+        wcp = ctx.enter_context(tc.tile_pool(name="wcp", bufs=2))
+        osp = ctx.enter_context(tc.tile_pool(name="osp", bufs=2))
+        psx = ctx.enter_context(tc.psum_pool(name="psx", bufs=4))
+        psa = ctx.enter_context(tc.psum_pool(name="psa", bufs=4))
+        ctx.enter_context(tc.manual_schedule())
+
+        a_view = alphas.rearrange("(p t) j k -> p t (j k)", t=PACK)
+        c_view = coeffs.rearrange("(p t) j k -> p t (j k)", t=PACK)
+        x_view = x.rearrange("(r b) i -> r (b i)", b=NB)
+        out_view = out.rearrange("(r b) j -> r b j", b=NB)
+
+        def load_chunk(view, c, label):
+            tl = acp.tile([P, PACK, JC * K], BF16, name=label, tag="ac")
+            nc.sync.dma_start(out=tl[:], in_=view[:, :, c * JC * K : (c + 1) * JC * K])
+            return tl
+
+        a_sb = [None] * NCH
+        c_sb = [None] * NCH
+        e_sb = [None] * NCH
+
+        a_sb[0] = load_chunk(a_view, 0, "a0")
+        x_sb = k8.tile([P, XW], BF16, name="x_sb", tag="k8", align_bytes=64)
+        nc.sync.dma_start(out=x_sb[:], in_=x_view)
+        for c in range(1, NCH):
+            a_sb[c] = load_chunk(a_view, c, "a%d" % c)
+        c_sb[0] = load_chunk(c_view, 0, "c0")
+
+        ident = const.tile([P, P], F32, name="ident")
+        make_identity(nc, ident[:])
+        probe = const.tile([P, 1], F32, name="probe")
+        nc.vector.memset(probe[:], 0.75)
+        probe_i = const.tile([P, 1], I32, name="probe_i")
+        nc.vector.tensor_copy(out=probe_i[:], in_=probe[:])
+        sin_scale = const.tile([P, 1], F32, name="sin_scale")
+        nc.vector.tensor_scalar(out=sin_scale[:], in0=probe_i[:], scalar1=2.0, scalar2=-1.0, op0=ALU.mult, op1=ALU.add)
+        sin_bias = const.tile([P, 1], F32, name="sin_bias")
+        nc.vector.tensor_scalar(out=sin_bias[:], in0=probe_i[:], scalar1=-math.pi, scalar2=math.pi, op0=ALU.mult, op1=ALU.add)
+
+        xg = keep.tile([P, XW], BF16, name="xg", align_bytes=64)
+        pc = keep.tile([P, NPRIM, NB * P], U32, name="pc", align_bytes=64)
+        ps = keep.tile([P, NPRIM, NB * P], U8, name="ps", align_bytes=64)
+
+        def max_sub(c):
+            a3 = a_sb[c][:].rearrange("p t (j k) -> p (t j) k", k=K)
+            m1 = mt.tile([P, PACK * JC, 4], BF16, name="m1")
+            nc.vector.tensor_tensor(out=m1[:], in0=a3[:, :, 0:4], in1=a3[:, :, 4:8], op=ALU.max)
+            m2 = mt.tile([P, PACK * JC, 2], BF16, name="m2")
+            nc.vector.tensor_tensor(out=m2[:], in0=m1[:, :, 0:2], in1=m1[:, :, 2:4], op=ALU.max)
+            m3 = mt.tile([P, JC, PACK], BF16, name="m3")
+            m2v = m2[:].rearrange("p (t j) k -> p j t k", t=PACK)
+            nc.vector.tensor_tensor(out=m3[:], in0=m2v[:, :, :, 0], in1=m2v[:, :, :, 1], op=ALU.max)
+            d = big.tile([P, K, JC, PACK], F32, name="e%d" % c, tag="k16")
+            nc.vector.tensor_tensor(
+                out=d[:],
+                in0=a_sb[c][:].rearrange("p t (j k) -> p k j t", k=K),
+                in1=m3[:].unsqueeze(1).to_broadcast([P, K, JC, PACK]),
+                op=ALU.subtract,
+            )
+            e_sb[c] = d
+
+        def exp_chunk(c):
+            flat = e_sb[c][:].rearrange("p k j t -> p (k j t)")
+            nc.scalar.activation(out=flat, in_=flat, func=ACT.Exp)
+
+        def quant_prim(k, src):
+            nc.vector.quantize_mx(out=pc[:, k, :].bitcast(FP8X4), scales=ps[:, k, :], in_=src)
+
+        def prim_tile(label):
+            return k8.tile([P, XW], BF16, name=label, tag="k8", align_bytes=64)
+
+        max_sub(0)
+        c_sb[1] = load_chunk(c_view, 1, "c1")
+
+        xw = x_sb[:].bitcast(F32).rearrange("p (b r u) -> p b u r", b=NB, u=2)
+        xgw = xg[:].bitcast(F32).rearrange("p (b r u) -> p b r u", b=NB, u=2)
+        for h in range(NB // 2):
+            xt = psx.tile([P, 2, 2, P], F32, name="xt")
+            for b2 in range(2):
+                for u in range(2):
+                    nc.tensor.transpose(xt[:, b2, u, :], xw[:, 2 * h + b2, u, :], ident[:])
+            nc.scalar.copy(out=xgw[:, 2 * h : 2 * h + 2, :, :], in_=xt[:].rearrange("p b u r -> p b r u"))
+
+        n_i = big.tile([P, XW], I32, name="n_i", tag="k16")
+        nc.vector.tensor_scalar(out=n_i[:], in0=xg[:], scalar1=0.5 / math.pi, scalar2=None, op0=ALU.mult)
+        y = big.tile([P, XW], F32, name="y", tag="k16")
+        nc.vector.scalar_tensor_tensor(out=y[:], in0=n_i[:], scalar=-2.0 * math.pi, in1=xg[:], op0=ALU.mult, op1=ALU.add)
+
+        lnx = big.tile([P, XW], F32, name="lnx", tag="k16")
+        nc.scalar.activation(out=lnx[:], in_=xg[:], func=ACT.Ln)
+        p_sin = prim_tile("p_sin")
+        nc.scalar.activation(out=p_sin[:], in_=y[:], func=ACT.Sin, bias=sin_bias[:], scale=sin_scale[:])
+
+        max_sub(1)
+        c_sb[2] = load_chunk(c_view, 2, "c2")
+        exp_chunk(0)
+        p_exp = prim_tile("p_exp")
+        nc.scalar.activation(out=p_exp[:], in_=xg[:], func=ACT.Exp)
+
+        max_sub(2)
+        c_sb[3] = load_chunk(c_view, 3, "c3")
+        p_sq = prim_tile("p_sq")
+        nc.vector.tensor_tensor(out=p_sq[:], in0=xg[:], in1=xg[:], op=ALU.mult)
+        quant_prim(0, xg[:])
+        quant_prim(6, p_sin[:])
+        quant_prim(1, p_sq[:])
+
+        exp_chunk(1)
+        p_rec = prim_tile("p_rec")
+        nc.scalar.activation(out=p_rec[:], in_=lnx[:], func=ACT.Exp, scale=-1.0)
+        p_cube = prim_tile("p_cube")
+        nc.scalar.activation(out=p_cube[:], in_=lnx[:], func=ACT.Exp, scale=3.0)
+
+        max_sub(3)
+        quant_prim(3, p_exp[:])
+        p_ln = prim_tile("p_ln")
+        nc.vector.tensor_copy(out=p_ln[:], in_=lnx[:])
+        quant_prim(5, p_rec[:])
+        quant_prim(4, p_ln[:])
+        quant_prim(2, p_cube[:])
+
+        exp_chunk(2)
+        exp_chunk(3)
+
+        sr = big.tile([P, 2, NCH, CW], F32, name="sr", tag="k16")
+        for c in range(NCH):
+            e3 = e_sb[c][:].rearrange("p k j t -> p k (j t)")
+            s4 = k8.tile([P, 4, CW], F32, name="s4", tag="k8", align_bytes=64)
+            nc.vector.tensor_tensor(out=s4[:], in0=e3[:, 0:4, :], in1=e3[:, 4:8, :], op=ALU.add)
+            s2 = mt.tile([P, 2, CW], F32, name="s2")
+            nc.vector.tensor_tensor(out=s2[:], in0=s4[:, 0:2, :], in1=s4[:, 2:4, :], op=ALU.add)
+            nc.vector.tensor_tensor(out=sr[:, 0, c, :], in0=s2[:, 0, :], in1=s2[:, 1, :], op=ALU.add)
+
+        s_all = sr[:, 0, :, :].rearrange("p c n -> p (c n)")
+        r_all = sr[:, 1, :, :].rearrange("p c n -> p (c n)")
+        nc.scalar.activation(out=s_all, in_=s_all, func=ACT.Ln)
+        nc.scalar.activation(out=r_all, in_=s_all, func=ACT.Exp, scale=-1.0)
+
+        for c in range(NCH):
+            nc.vector.tensor_tensor(
+                out=e_sb[c][:, 1:K],
+                in0=e_sb[c][:, 1:K],
+                in1=c_sb[c][:].rearrange("p t (j k) -> p k j t", k=K)[:, 1:K],
+                op=ALU.mult,
+            )
+
+        wq = [None] * NCH
+        wc = [None] * NCH
+        ws = [None] * NCH
+
+        def scale_chunk(c):
+            wq[c] = k8.tile([P, NPRIM, CW], BF16, name="wq", tag="k8", align_bytes=64)
+            nc.vector.tensor_tensor(
+                out=wq[c][:],
+                in0=e_sb[c][:, 1:K].rearrange("p k j t -> p k (j t)"),
+                in1=sr[:, 1, c, :].unsqueeze(1).to_broadcast([P, NPRIM, CW]),
+                op=ALU.mult,
+            )
+
+        def quant_chunk(c):
+            wc[c] = wcp.tile([P, NPRIM * JC], U32, name="wc", align_bytes=64)
+            ws[c] = wcp.tile([P, NPRIM * JC], U8, name="ws", align_bytes=64)
+            flat = wq[c][:].rearrange("p k n -> p (k n)")
+            for lo, hi in ((0, 4), (4, 6), (6, 7)):
+                nc.vector.quantize_mx(
+                    out=wc[c][:, lo * JC : hi * JC].bitcast(FP8X4),
+                    scales=ws[c][:, lo * JC : hi * JC],
+                    in_=flat[:, lo * CW : hi * CW],
+                )
+
+        def multiply_chunk(c):
+            ost = osp.tile([P, NB, JC], F32, name="ost")
+            for h in range(2):
+                acc = psa.tile([P, 4, JC], F32, name="acc")
+                for b4 in range(4):
+                    bt = 4 * h + b4
+                    for k in range(NPRIM):
+                        nc.tensor.matmul_mx(
+                            out=acc[:, b4, :],
+                            lhsT=pc[:, k, bt * P : (bt + 1) * P].bitcast(FP8X4),
+                            lhsT_scale=ps[:, k, bt * P : (bt + 1) * P],
+                            rhs=wc[c][:, k * JC : (k + 1) * JC].bitcast(FP8X4),
+                            rhs_scale=ws[c][:, k * JC : (k + 1) * JC],
+                            start=(k == 0),
+                            stop=(k == NPRIM - 1),
+                        )
+                nc.scalar.copy(out=ost[:, 4 * h : 4 * h + 4, :], in_=acc[:])
+            nc.sync.dma_start(out=out_view[:, :, c * JC : (c + 1) * JC], in_=ost[:])
+
+        scale_chunk(0)
+        scale_chunk(1)
+        quant_chunk(0)
+        multiply_chunk(0)
+        scale_chunk(2)
+        quant_chunk(1)
+        multiply_chunk(1)
+        scale_chunk(3)
+        quant_chunk(2)
+        multiply_chunk(2)
+        quant_chunk(3)
+        multiply_chunk(3)

@@ -37,7 +37,7 @@ def tile_dartslayer_kernel(tc, x, alphas, coeffs, out):
         mt = ctx.enter_context(tc.tile_pool(name="mt", bufs=1))
         wcp = ctx.enter_context(tc.tile_pool(name="wcp", bufs=2))
         osp = ctx.enter_context(tc.tile_pool(name="osp", bufs=2))
-        psx = ctx.enter_context(tc.psum_pool(name="psx", bufs=4))
+        ps4 = ctx.enter_context(tc.psum_pool(name="ps4", bufs=4))
         psa = ctx.enter_context(tc.psum_pool(name="psa", bufs=4))
         ctx.enter_context(tc.manual_schedule())
 
@@ -86,18 +86,43 @@ def tile_dartslayer_kernel(tc, x, alphas, coeffs, out):
             m3 = mt.tile([P, JC, PACK], BF16, name="m3")
             m2v = m2[:].rearrange("p (t j) k -> p j t k", t=PACK)
             nc.vector.tensor_tensor(out=m3[:], in0=m2v[:, :, :, 0], in1=m2v[:, :, :, 1], op=ALU.max)
-            d = big.tile([P, K, JC, PACK], F32, name="e%d" % c, tag="k16")
+            d = big.tile([P, JC, PACK, K], F32, name="e%d" % c, tag="k16")
             nc.vector.tensor_tensor(
                 out=d[:],
-                in0=a_sb[c][:].rearrange("p t (j k) -> p k j t", k=K),
-                in1=m3[:].unsqueeze(1).to_broadcast([P, K, JC, PACK]),
+                in0=a_sb[c][:].rearrange("p t (j k) -> p j t k", k=K),
+                in1=m3[:].unsqueeze(3).to_broadcast([P, JC, PACK, K]),
                 op=ALU.subtract,
             )
             e_sb[c] = d
 
         def exp_chunk(c):
-            flat = e_sb[c][:].rearrange("p k j t -> p (k j t)")
+            flat = e_sb[c][:].rearrange("p j t k -> p (j t k)")
             nc.scalar.activation(out=flat, in_=flat, func=ACT.Exp)
+
+        st = [None] * NCH
+        rr = [None] * NCH
+
+        def sum_chunk(c):
+            e2 = e_sb[c][:].rearrange("p j t k -> p (j t) k")
+            st[c] = ps4.tile([P, PACK, P], F32, name="st", tag="t4")
+            for q in range(PACK):
+                for k in range(K):
+                    nc.tensor.matmul(
+                        out=st[c][:, q, :],
+                        lhsT=e2[:, q * P : (q + 1) * P, k],
+                        rhs=ident[:],
+                        is_transpose=True,
+                        start=(k == 0),
+                        stop=(k == K - 1),
+                    )
+
+        def times_coeffs(c):
+            nc.vector.tensor_tensor(
+                out=e_sb[c][:, :, :, 1:K],
+                in0=e_sb[c][:, :, :, 1:K],
+                in1=c_sb[c][:].rearrange("p t (j k) -> p j t k", k=K)[:, :, :, 1:K],
+                op=ALU.mult,
+            )
 
         def quant_prim(k, src):
             nc.vector.quantize_mx(out=pc[:, k, :].bitcast(FP8X4), scales=ps[:, k, :], in_=src)
@@ -111,7 +136,7 @@ def tile_dartslayer_kernel(tc, x, alphas, coeffs, out):
         xw = x_sb[:].bitcast(F32).rearrange("p (b r u) -> p b u r", b=NB, u=2)
         xgw = xg[:].bitcast(F32).rearrange("p (b r u) -> p b r u", b=NB, u=2)
         for h in range(NB // 2):
-            xt = psx.tile([P, 2, 2, P], F32, name="xt")
+            xt = ps4.tile([P, 2, 2, P], F32, name="xt", tag="t4")
             for b2 in range(2):
                 for u in range(2):
                     nc.tensor.transpose(xt[:, b2, u, :], xw[:, 2 * h + b2, u, :], ident[:])
@@ -130,79 +155,69 @@ def tile_dartslayer_kernel(tc, x, alphas, coeffs, out):
         max_sub(1)
         c_sb[2] = load_chunk(c_view, 2, "c2")
         exp_chunk(0)
+        sum_chunk(0)
+        max_sub(2)
+        c_sb[3] = load_chunk(c_view, 3, "c3")
+        exp_chunk(1)
+        sum_chunk(1)
+        max_sub(3)
+        exp_chunk(2)
+        sum_chunk(2)
+        exp_chunk(3)
+        sum_chunk(3)
         p_exp = prim_tile("p_exp")
         nc.scalar.activation(out=p_exp[:], in_=xg[:], func=ACT.Exp)
 
-        max_sub(2)
-        c_sb[3] = load_chunk(c_view, 3, "c3")
         p_sq = prim_tile("p_sq")
         nc.vector.tensor_tensor(out=p_sq[:], in0=xg[:], in1=xg[:], op=ALU.mult)
         quant_prim(0, xg[:])
         quant_prim(6, p_sin[:])
         quant_prim(1, p_sq[:])
+        p_ln = prim_tile("p_ln")
+        nc.vector.tensor_copy(out=p_ln[:], in_=lnx[:])
+        times_coeffs(0)
+        quant_prim(4, p_ln[:])
+        times_coeffs(1)
+        quant_prim(3, p_exp[:])
+        times_coeffs(2)
 
-        exp_chunk(1)
+        lnst = k8.tile([P, NCH, CW], F32, name="lnst", tag="k8", align_bytes=64)
+        for c in range(NCH):
+            nc.scalar.activation(out=lnst[:, c, :], in_=st[c][:].rearrange("p q n -> p (q n)"), func=ACT.Ln)
+        rt = k8.tile([P, NCH, CW], F32, name="rt", tag="k8", align_bytes=64)
+        nc.scalar.activation(
+            out=rt[:].rearrange("p c n -> p (c n)"), in_=lnst[:].rearrange("p c n -> p (c n)"), func=ACT.Exp, scale=-1.0
+        )
+        for c in range(NCH):
+            rr[c] = ps4.tile([P, PACK, P], F32, name="rr", tag="t4")
+            for q in range(PACK):
+                nc.tensor.transpose(rr[c][:, q, :], rt[:, c, q * P : (q + 1) * P], ident[:])
+
         p_rec = prim_tile("p_rec")
         nc.scalar.activation(out=p_rec[:], in_=lnx[:], func=ACT.Exp, scale=-1.0)
         p_cube = prim_tile("p_cube")
         nc.scalar.activation(out=p_cube[:], in_=lnx[:], func=ACT.Exp, scale=3.0)
 
-        max_sub(3)
-        quant_prim(3, p_exp[:])
-        p_ln = prim_tile("p_ln")
-        nc.vector.tensor_copy(out=p_ln[:], in_=lnx[:])
-        quant_prim(5, p_rec[:])
-        quant_prim(4, p_ln[:])
-        quant_prim(2, p_cube[:])
-
-        exp_chunk(2)
-        exp_chunk(3)
-
-        sr = big.tile([P, 2, NCH, CW], F32, name="sr", tag="k16")
-        for c in range(NCH):
-            e3 = e_sb[c][:].rearrange("p k j t -> p k (j t)")
-            s4 = k8.tile([P, 4, CW], F32, name="s4", tag="k8", align_bytes=64)
-            nc.vector.tensor_tensor(out=s4[:], in0=e3[:, 0:4, :], in1=e3[:, 4:8, :], op=ALU.add)
-            s2 = mt.tile([P, 2, CW], F32, name="s2")
-            nc.vector.tensor_tensor(out=s2[:], in0=s4[:, 0:2, :], in1=s4[:, 2:4, :], op=ALU.add)
-            nc.vector.tensor_tensor(out=sr[:, 0, c, :], in0=s2[:, 0, :], in1=s2[:, 1, :], op=ALU.add)
-
-        s_all = sr[:, 0, :, :].rearrange("p c n -> p (c n)")
-        r_all = sr[:, 1, :, :].rearrange("p c n -> p (c n)")
-        nc.scalar.activation(out=s_all, in_=s_all, func=ACT.Ln)
-        nc.scalar.activation(out=r_all, in_=s_all, func=ACT.Exp, scale=-1.0)
-
-        for c in range(NCH):
-            nc.vector.tensor_tensor(
-                out=e_sb[c][:, 1:K],
-                in0=e_sb[c][:, 1:K],
-                in1=c_sb[c][:].rearrange("p t (j k) -> p k j t", k=K)[:, 1:K],
-                op=ALU.mult,
-            )
-
         wq = [None] * NCH
         wc = [None] * NCH
         ws = [None] * NCH
+        LO = 4
 
-        def scale_chunk(c):
-            wq[c] = k8.tile([P, NPRIM, CW], BF16, name="wq", tag="k8", align_bytes=64)
+        def scale_part(c, lo, hi):
             nc.vector.tensor_tensor(
-                out=wq[c][:],
-                in0=e_sb[c][:, 1:K].rearrange("p k j t -> p k (j t)"),
-                in1=sr[:, 1, c, :].unsqueeze(1).to_broadcast([P, NPRIM, CW]),
+                out=wq[c][:].rearrange("p k n -> p n k")[:, :, lo:hi],
+                in0=e_sb[c][:].rearrange("p j t k -> p (j t) k")[:, :, lo + 1 : hi + 1],
+                in1=rr[c][:].rearrange("p q n -> p (q n)").unsqueeze(2).to_broadcast([P, CW, hi - lo]),
                 op=ALU.mult,
             )
 
-        def quant_chunk(c):
-            wc[c] = wcp.tile([P, NPRIM * JC], U32, name="wc", align_bytes=64)
-            ws[c] = wcp.tile([P, NPRIM * JC], U8, name="ws", align_bytes=64)
+        def quant_part(c, lo, hi):
             flat = wq[c][:].rearrange("p k n -> p (k n)")
-            for lo, hi in ((0, 4), (4, 6), (6, 7)):
-                nc.vector.quantize_mx(
-                    out=wc[c][:, lo * JC : hi * JC].bitcast(FP8X4),
-                    scales=ws[c][:, lo * JC : hi * JC],
-                    in_=flat[:, lo * CW : hi * CW],
-                )
+            nc.vector.quantize_mx(
+                out=wc[c][:, lo * JC : hi * JC].bitcast(FP8X4),
+                scales=ws[c][:, lo * JC : hi * JC],
+                in_=flat[:, lo * CW : hi * CW],
+            )
 
         def multiply_chunk(c):
             ost = osp.tile([P, NB, JC], F32, name="ost")
@@ -223,15 +238,19 @@ def tile_dartslayer_kernel(tc, x, alphas, coeffs, out):
                 nc.scalar.copy(out=ost[:, 4 * h : 4 * h + 4, :], in_=acc[:])
             nc.sync.dma_start(out=out_view[:, :, c * JC : (c + 1) * JC], in_=ost[:])
 
-        scale_chunk(0)
-        scale_chunk(1)
-        quant_chunk(0)
-        multiply_chunk(0)
-        scale_chunk(2)
-        quant_chunk(1)
-        multiply_chunk(1)
-        scale_chunk(3)
-        quant_chunk(2)
-        multiply_chunk(2)
-        quant_chunk(3)
-        multiply_chunk(3)
+        for c in range(NCH):
+            wq[c] = k8.tile([P, NPRIM, CW], BF16, name="wq", tag="k8", align_bytes=64)
+            wc[c] = wcp.tile([P, NPRIM * JC], U32, name="wc", align_bytes=64)
+            ws[c] = wcp.tile([P, NPRIM * JC], U8, name="ws", align_bytes=64)
+            scale_part(c, 0, LO)
+            scale_part(c, LO, NPRIM)
+            quant_part(c, 0, 4)
+            if c == 0:
+                quant_prim(5, p_rec[:])
+            quant_part(c, 4, 6)
+            quant_part(c, 6, 7)
+            if c == 0:
+                quant_prim(2, p_cube[:])
+            multiply_chunk(c)
+            if c == 0:
+                times_coeffs(3)

@@ -22,6 +22,8 @@ NCH = J // JC
 NPRIM = K - 1
 XW = NB * P * PACK
 CW = JC * PACK
+TJ = 16
+HALF = JC // 2
 
 FLOPS = 2 * B * I * J * NPRIM
 
@@ -30,13 +32,13 @@ def tile_dartslayer_kernel(tc, x, alphas, coeffs, out):
     nc = tc.nc
     with ExitStack() as ctx:
         const = ctx.enter_context(tc.tile_pool(name="const", bufs=1))
-        big = ctx.enter_context(tc.tile_pool(name="big", bufs=5))
-        acp = ctx.enter_context(tc.tile_pool(name="acp", bufs=5))
+        big = ctx.enter_context(tc.tile_pool(name="big", bufs=6))
+        acp = ctx.enter_context(tc.tile_pool(name="acp", bufs=4))
         k8 = ctx.enter_context(tc.tile_pool(name="k8", bufs=4))
         keep = ctx.enter_context(tc.tile_pool(name="keep", bufs=1))
         mt = ctx.enter_context(tc.tile_pool(name="mt", bufs=1))
         wcp = ctx.enter_context(tc.tile_pool(name="wcp", bufs=2))
-        osp = ctx.enter_context(tc.tile_pool(name="osp", bufs=2))
+        osp = ctx.enter_context(tc.tile_pool(name="osp", bufs=4))
         ps4 = ctx.enter_context(tc.psum_pool(name="ps4", bufs=4))
         psa = ctx.enter_context(tc.psum_pool(name="psa", bufs=4))
         ctx.enter_context(tc.manual_schedule())
@@ -46,24 +48,34 @@ def tile_dartslayer_kernel(tc, x, alphas, coeffs, out):
         x_view = x.rearrange("(r b) i -> r (b i)", b=NB)
         out_view = out.rearrange("(r b) j -> r b j", b=NB)
 
-        def load_chunk(view, c, label):
+        def load_chunk(view, c, label, pieces):
             tl = acp.tile([P, PACK, JC * K], BF16, name=label, tag="ac")
-            nc.sync.dma_start(out=tl[:], in_=view[:, :, c * JC * K : (c + 1) * JC * K])
+            w = JC * K // pieces
+            for h in range(pieces):
+                nc.sync.dma_start(
+                    out=tl[:, :, h * w : (h + 1) * w], in_=view[:, :, c * JC * K + h * w : c * JC * K + (h + 1) * w]
+                )
             return tl
 
         a_sb = [None] * NCH
         c_sb = [None] * NCH
         e_sb = [None] * NCH
+        st = [None] * NCH
+        rr = [None] * NCH
 
-        a_sb[0] = load_chunk(a_view, 0, "a0")
+        a_sb[0] = load_chunk(a_view, 0, "a0", 2)
+        a_sb[1] = load_chunk(a_view, 1, "a1", 2)
         x_sb = k8.tile([P, XW], BF16, name="x_sb", tag="k8", align_bytes=64)
         nc.sync.dma_start(out=x_sb[:], in_=x_view)
-        for c in range(1, NCH):
-            a_sb[c] = load_chunk(a_view, c, "a%d" % c)
-        c_sb[0] = load_chunk(c_view, 0, "c0")
+        a_sb[2] = load_chunk(a_view, 2, "a2", 1)
+        a_sb[3] = load_chunk(a_view, 3, "a3", 1)
 
         ident = const.tile([P, P], F32, name="ident")
         make_identity(nc, ident[:])
+        ident_bf = const.tile([P, P], BF16, name="ident_bf")
+        nc.vector.tensor_copy(out=ident_bf[:], in_=ident[:])
+        neg_bf = const.tile([P, P], BF16, name="neg_bf")
+        nc.vector.tensor_scalar(out=neg_bf[:], in0=ident[:], scalar1=-1.0, scalar2=None, op0=ALU.mult)
         probe = const.tile([P, 1], F32, name="probe")
         nc.vector.memset(probe[:], 0.75)
         probe_i = const.tile([P, 1], I32, name="probe_i")
@@ -77,30 +89,40 @@ def tile_dartslayer_kernel(tc, x, alphas, coeffs, out):
         pc = keep.tile([P, NPRIM, NB * P], U32, name="pc", align_bytes=64)
         ps = keep.tile([P, NPRIM, NB * P], U8, name="ps", align_bytes=64)
 
-        def max_sub(c):
-            a3 = a_sb[c][:].rearrange("p t (j k) -> p (t j) k", k=K)
-            m1 = mt.tile([P, PACK * JC, 4], BF16, name="m1")
-            nc.vector.tensor_tensor(out=m1[:], in0=a3[:, :, 0:4], in1=a3[:, :, 4:8], op=ALU.max)
-            m2 = mt.tile([P, PACK * JC, 2], BF16, name="m2")
-            nc.vector.tensor_tensor(out=m2[:], in0=m1[:, :, 0:2], in1=m1[:, :, 2:4], op=ALU.max)
-            m3 = mt.tile([P, JC, PACK], BF16, name="m3")
-            m2v = m2[:].rearrange("p (t j) k -> p j t k", t=PACK)
+        def new_e(c):
+            e_sb[c] = big.tile([P, JC, PACK, K], F32, name="e%d" % c, tag="k16")
+
+        def a_by_j(c):
+            return a_sb[c][:].rearrange("p t (j k) -> p j t k", k=K)
+
+        def tree(c, j0, nj):
+            a4 = a_sb[c][:].rearrange("p t (j k) -> p t j k", k=K)[:, :, j0 : j0 + nj, :]
+            m1 = mt.tile([P, PACK, nj, 4], BF16, name="m1")
+            nc.vector.tensor_tensor(out=m1[:], in0=a4[:, :, :, 0:4], in1=a4[:, :, :, 4:8], op=ALU.max)
+            m2 = mt.tile([P, PACK, nj, 2], BF16, name="m2")
+            nc.vector.tensor_tensor(out=m2[:], in0=m1[:, :, :, 0:2], in1=m1[:, :, :, 2:4], op=ALU.max)
+            m3 = mt.tile([P, nj, PACK], BF16, name="m3", bufs=3)
+            m2v = m2[:].rearrange("p t j k -> p j t k")
             nc.vector.tensor_tensor(out=m3[:], in0=m2v[:, :, :, 0], in1=m2v[:, :, :, 1], op=ALU.max)
-            d = big.tile([P, JC, PACK, K], F32, name="e%d" % c, tag="k16")
+            return m3
+
+        def spread(m3, off, nj):
+            return m3[:, off : off + nj, :].unsqueeze(3).to_broadcast([P, nj, PACK, K])
+
+        def sub_vector(c, m3, j0, nj, off):
             nc.vector.tensor_tensor(
-                out=d[:],
-                in0=a_sb[c][:].rearrange("p t (j k) -> p j t k", k=K),
-                in1=m3[:].unsqueeze(3).to_broadcast([P, JC, PACK, K]),
-                op=ALU.subtract,
+                out=e_sb[c][:, j0 : j0 + nj], in0=a_by_j(c)[:, j0 : j0 + nj], in1=spread(m3, off, nj), op=ALU.subtract
             )
-            e_sb[c] = d
 
-        def exp_chunk(c):
-            flat = e_sb[c][:].rearrange("p j t k -> p (j t k)")
+        def sub_exp_tensor(c, m3, j0, off):
+            dps = psa.tile([P, TJ, PACK, K], F32, name="dps", tag="acc")
+            nc.tensor.matmul(out=dps[:], lhsT=ident_bf[:], rhs=a_by_j(c)[:, j0 : j0 + TJ], start=True, stop=False)
+            nc.tensor.matmul(out=dps[:], lhsT=neg_bf[:], rhs=spread(m3, off, TJ), start=False, stop=True)
+            nc.scalar.activation(out=e_sb[c][:, j0 : j0 + TJ], in_=dps[:], func=ACT.Exp)
+
+        def exp_sbuf(c, j0, nj):
+            flat = e_sb[c][:, j0 : j0 + nj].rearrange("p j t k -> p (j t k)")
             nc.scalar.activation(out=flat, in_=flat, func=ACT.Exp)
-
-        st = [None] * NCH
-        rr = [None] * NCH
 
         def sum_chunk(c):
             e2 = e_sb[c][:].rearrange("p j t k -> p (j t) k")
@@ -130,8 +152,21 @@ def tile_dartslayer_kernel(tc, x, alphas, coeffs, out):
         def prim_tile(label):
             return k8.tile([P, XW], BF16, name=label, tag="k8", align_bytes=64)
 
-        max_sub(0)
-        c_sb[1] = load_chunk(c_view, 1, "c1")
+        new_e(0)
+        for h in range(2):
+            m3 = tree(0, h * HALF, HALF)
+            for q in range(HALF // TJ):
+                sub_exp_tensor(0, m3, h * HALF + q * TJ, q * TJ)
+        c_sb[0] = load_chunk(c_view, 0, "c0", 1)
+
+        new_e(1)
+        m3 = tree(1, 0, HALF)
+        sub_exp_tensor(1, m3, 0, 0)
+        sub_exp_tensor(1, m3, TJ, TJ)
+        sub_vector(1, m3, 2 * TJ, HALF - 2 * TJ, 2 * TJ)
+        m3 = tree(1, HALF, HALF)
+        sub_vector(1, m3, HALF, HALF, 0)
+        c_sb[1] = load_chunk(c_view, 1, "c1", 1)
 
         xw = x_sb[:].bitcast(F32).rearrange("p (b r u) -> p b u r", b=NB, u=2)
         xgw = xg[:].bitcast(F32).rearrange("p (b r u) -> p b r u", b=NB, u=2)
@@ -142,52 +177,49 @@ def tile_dartslayer_kernel(tc, x, alphas, coeffs, out):
                     nc.tensor.transpose(xt[:, b2, u, :], xw[:, 2 * h + b2, u, :], ident[:])
             nc.scalar.copy(out=xgw[:, 2 * h : 2 * h + 2, :, :], in_=xt[:].rearrange("p b u r -> p b r u"))
 
+        sum_chunk(0)
+        exp_sbuf(1, 2 * TJ, JC - 2 * TJ)
+        sum_chunk(1)
+
+        new_e(2)
+        m3 = tree(2, 0, JC)
+        sub_vector(2, m3, 0, JC, 0)
+        c_sb[2] = load_chunk(c_view, 2, "c2", 1)
+        p_exp = prim_tile("p_exp")
+        nc.scalar.activation(out=p_exp[:], in_=xg[:], func=ACT.Exp)
+        exp_sbuf(2, 0, JC)
+        sum_chunk(2)
+
+        new_e(3)
+        m3 = tree(3, 0, JC)
+        sub_vector(3, m3, 0, JC, 0)
+        c_sb[3] = load_chunk(c_view, 3, "c3", 1)
+        exp_sbuf(3, 0, JC)
+        sum_chunk(3)
+
         n_i = big.tile([P, XW], I32, name="n_i", tag="k16")
         nc.vector.tensor_scalar(out=n_i[:], in0=xg[:], scalar1=0.5 / math.pi, scalar2=None, op0=ALU.mult)
         y = big.tile([P, XW], F32, name="y", tag="k16")
         nc.vector.scalar_tensor_tensor(out=y[:], in0=n_i[:], scalar=-2.0 * math.pi, in1=xg[:], op0=ALU.mult, op1=ALU.add)
-
-        lnx = big.tile([P, XW], F32, name="lnx", tag="k16")
-        nc.scalar.activation(out=lnx[:], in_=xg[:], func=ACT.Ln)
         p_sin = prim_tile("p_sin")
         nc.scalar.activation(out=p_sin[:], in_=y[:], func=ACT.Sin, bias=sin_bias[:], scale=sin_scale[:])
-
-        max_sub(1)
-        c_sb[2] = load_chunk(c_view, 2, "c2")
-        exp_chunk(0)
-        sum_chunk(0)
-        max_sub(2)
-        c_sb[3] = load_chunk(c_view, 3, "c3")
-        exp_chunk(1)
-        sum_chunk(1)
-        max_sub(3)
-        exp_chunk(2)
-        sum_chunk(2)
-        exp_chunk(3)
-        sum_chunk(3)
-        p_exp = prim_tile("p_exp")
-        nc.scalar.activation(out=p_exp[:], in_=xg[:], func=ACT.Exp)
 
         p_sq = prim_tile("p_sq")
         nc.vector.tensor_tensor(out=p_sq[:], in0=xg[:], in1=xg[:], op=ALU.mult)
         quant_prim(0, xg[:])
-        quant_prim(6, p_sin[:])
-        quant_prim(1, p_sq[:])
-        p_ln = prim_tile("p_ln")
-        nc.vector.tensor_copy(out=p_ln[:], in_=lnx[:])
-        times_coeffs(0)
-        quant_prim(4, p_ln[:])
-        times_coeffs(1)
         quant_prim(3, p_exp[:])
-        times_coeffs(2)
+        quant_prim(1, p_sq[:])
+        times_coeffs(0)
+        times_coeffs(1)
+        quant_prim(6, p_sin[:])
 
-        lnst = k8.tile([P, NCH, CW], F32, name="lnst", tag="k8", align_bytes=64)
-        for c in range(NCH):
-            nc.scalar.activation(out=lnst[:, c, :], in_=st[c][:].rearrange("p q n -> p (q n)"), func=ACT.Ln)
+        lnx = big.tile([P, XW], F32, name="lnx", tag="k16")
+        nc.scalar.activation(out=lnx[:], in_=xg[:], func=ACT.Ln)
         rt = k8.tile([P, NCH, CW], F32, name="rt", tag="k8", align_bytes=64)
-        nc.scalar.activation(
-            out=rt[:].rearrange("p c n -> p (c n)"), in_=lnst[:].rearrange("p c n -> p (c n)"), func=ACT.Exp, scale=-1.0
-        )
+        for c in range(NCH):
+            nc.scalar.activation(out=rt[:, c, :], in_=st[c][:].rearrange("p q n -> p (q n)"), func=ACT.Ln)
+        rt_flat = rt[:].rearrange("p c n -> p (c n)")
+        nc.scalar.activation(out=rt_flat, in_=rt_flat, func=ACT.Exp, scale=-1.0)
         for c in range(NCH):
             rr[c] = ps4.tile([P, PACK, P], F32, name="rr", tag="t4")
             for q in range(PACK):
@@ -197,6 +229,12 @@ def tile_dartslayer_kernel(tc, x, alphas, coeffs, out):
         nc.scalar.activation(out=p_rec[:], in_=lnx[:], func=ACT.Exp, scale=-1.0)
         p_cube = prim_tile("p_cube")
         nc.scalar.activation(out=p_cube[:], in_=lnx[:], func=ACT.Exp, scale=3.0)
+
+        times_coeffs(2)
+        p_ln = prim_tile("p_ln")
+        nc.vector.tensor_copy(out=p_ln[:], in_=lnx[:])
+        times_coeffs(3)
+        quant_prim(4, p_ln[:])
 
         wq = [None] * NCH
         wc = [None] * NCH
@@ -220,9 +258,8 @@ def tile_dartslayer_kernel(tc, x, alphas, coeffs, out):
             )
 
         def multiply_chunk(c):
-            ost = osp.tile([P, NB, JC], F32, name="ost")
             for h in range(2):
-                acc = psa.tile([P, 4, JC], F32, name="acc")
+                acc = psa.tile([P, 4, JC], F32, name="acc", tag="acc")
                 for b4 in range(4):
                     bt = 4 * h + b4
                     for k in range(NPRIM):
@@ -235,8 +272,9 @@ def tile_dartslayer_kernel(tc, x, alphas, coeffs, out):
                             start=(k == 0),
                             stop=(k == NPRIM - 1),
                         )
-                nc.scalar.copy(out=ost[:, 4 * h : 4 * h + 4, :], in_=acc[:])
-            nc.sync.dma_start(out=out_view[:, :, c * JC : (c + 1) * JC], in_=ost[:])
+                ost = osp.tile([P, 4, JC], F32, name="ost")
+                nc.scalar.copy(out=ost[:], in_=acc[:])
+                nc.sync.dma_start(out=out_view[:, 4 * h : 4 * h + 4, c * JC : (c + 1) * JC], in_=ost[:])
 
         for c in range(NCH):
             wq[c] = k8.tile([P, NPRIM, CW], BF16, name="wq", tag="k8", align_bytes=64)
@@ -252,5 +290,3 @@ def tile_dartslayer_kernel(tc, x, alphas, coeffs, out):
             if c == 0:
                 quant_prim(2, p_cube[:])
             multiply_chunk(c)
-            if c == 0:
-                times_coeffs(3)

@@ -62,6 +62,7 @@ def tile_dartslayer_kernel(tc, x, alphas, coeffs, out):
         e_sb = [None] * NCH
         st = [None] * NCH
         rr = [None] * NCH
+        tt = [None] * NCH
 
         a_sb[0] = load_chunk(a_view, 0, "a0", 2)
         a_sb[1] = load_chunk(a_view, 1, "a1", 2)
@@ -96,14 +97,15 @@ def tile_dartslayer_kernel(tc, x, alphas, coeffs, out):
             return a_sb[c][:].rearrange("p t (j k) -> p j t k", k=K)
 
         def tree(c, j0, nj):
-            a4 = a_sb[c][:].rearrange("p t (j k) -> p t j k", k=K)[:, :, j0 : j0 + nj, :]
-            m1 = mt.tile([P, PACK, nj, 4], BF16, name="m1")
-            nc.vector.tensor_tensor(out=m1[:], in0=a4[:, :, :, 0:4], in1=a4[:, :, :, 4:8], op=ALU.max)
-            m2 = mt.tile([P, PACK, nj, 2], BF16, name="m2")
-            nc.vector.tensor_tensor(out=m2[:], in0=m1[:, :, :, 0:2], in1=m1[:, :, :, 2:4], op=ALU.max)
+            a6 = a_sb[c][:].rearrange("p t (j g h e) -> p g j t h e", g=2, h=2, e=2)[:, :, j0 : j0 + nj]
+            m1 = mt.tile([P, 2, nj, PACK, 2], BF16, name="m1")
+            nc.vector.tensor_tensor(
+                out=m1[:].rearrange("p h j t e -> p j t h e"), in0=a6[:, 0], in1=a6[:, 1], op=ALU.max
+            )
+            m2 = mt.tile([P, nj, PACK, 2], BF16, name="m2")
+            nc.vector.tensor_tensor(out=m2[:], in0=m1[:, 0], in1=m1[:, 1], op=ALU.max)
             m3 = mt.tile([P, nj, PACK], BF16, name="m3", bufs=3)
-            m2v = m2[:].rearrange("p t j k -> p j t k")
-            nc.vector.tensor_tensor(out=m3[:], in0=m2v[:, :, :, 0], in1=m2v[:, :, :, 1], op=ALU.max)
+            nc.vector.tensor_tensor(out=m3[:], in0=m2[:, :, :, 0], in1=m2[:, :, :, 1], op=ALU.max)
             return m3
 
         def spread(m3, off, nj):
@@ -139,12 +141,13 @@ def tile_dartslayer_kernel(tc, x, alphas, coeffs, out):
                     )
 
         def times_coeffs(c):
-            nc.vector.tensor_tensor(
-                out=e_sb[c][:, :, :, 1:K],
-                in0=e_sb[c][:, :, :, 1:K],
-                in1=c_sb[c][:].rearrange("p t (j k) -> p j t k", k=K)[:, :, :, 1:K],
-                op=ALU.mult,
-            )
+            tt[c] = big.tile([P, NPRIM, CW], F32, name="tt%d" % c, tag="k16")
+            planes = tt[c][:].rearrange("p k (j t) -> p j t k", t=PACK)
+            c4 = c_sb[c][:].rearrange("p t (j k) -> p j t k", k=K)
+            for lo, hi in ((1, 4), (4, K)):
+                nc.vector.tensor_tensor(
+                    out=planes[:, :, :, lo - 1 : hi - 1], in0=e_sb[c][:, :, :, lo:hi], in1=c4[:, :, :, lo:hi], op=ALU.mult
+                )
 
         def quant_prim(k, src):
             nc.vector.quantize_mx(out=pc[:, k, :].bitcast(FP8X4), scales=ps[:, k, :], in_=src)
@@ -210,11 +213,11 @@ def tile_dartslayer_kernel(tc, x, alphas, coeffs, out):
         quant_prim(3, p_exp[:])
         quant_prim(1, p_sq[:])
         times_coeffs(0)
+        lnx = big.tile([P, XW], F32, name="lnx", tag="k16")
+        nc.scalar.activation(out=lnx[:], in_=xg[:], func=ACT.Ln)
         times_coeffs(1)
         quant_prim(6, p_sin[:])
 
-        lnx = big.tile([P, XW], F32, name="lnx", tag="k16")
-        nc.scalar.activation(out=lnx[:], in_=xg[:], func=ACT.Ln)
         rt = k8.tile([P, NCH, CW], F32, name="rt", tag="k8", align_bytes=64)
         for c in range(NCH):
             nc.scalar.activation(out=rt[:, c, :], in_=st[c][:].rearrange("p q n -> p (q n)"), func=ACT.Ln)
@@ -243,9 +246,9 @@ def tile_dartslayer_kernel(tc, x, alphas, coeffs, out):
 
         def scale_part(c, lo, hi):
             nc.vector.tensor_tensor(
-                out=wq[c][:].rearrange("p k n -> p n k")[:, :, lo:hi],
-                in0=e_sb[c][:].rearrange("p j t k -> p (j t) k")[:, :, lo + 1 : hi + 1],
-                in1=rr[c][:].rearrange("p q n -> p (q n)").unsqueeze(2).to_broadcast([P, CW, hi - lo]),
+                out=wq[c][:, lo:hi, :],
+                in0=tt[c][:, lo:hi, :],
+                in1=rr[c][:].rearrange("p q n -> p (q n)").unsqueeze(1).to_broadcast([P, hi - lo, CW]),
                 op=ALU.mult,
             )
 

@@ -33,10 +33,10 @@ def tile_dartslayer_kernel(tc, x, alphas, coeffs, out):
     with ExitStack() as ctx:
         const = ctx.enter_context(tc.tile_pool(name="const", bufs=1))
         big = ctx.enter_context(tc.tile_pool(name="big", bufs=6))
-        acp = ctx.enter_context(tc.tile_pool(name="acp", bufs=4))
+        acp = ctx.enter_context(tc.tile_pool(name="acp", bufs=3))
         k8 = ctx.enter_context(tc.tile_pool(name="k8", bufs=4))
         keep = ctx.enter_context(tc.tile_pool(name="keep", bufs=1))
-        mt = ctx.enter_context(tc.tile_pool(name="mt", bufs=1))
+        mt = ctx.enter_context(tc.tile_pool(name="mt", bufs=2))
         wcp = ctx.enter_context(tc.tile_pool(name="wcp", bufs=2))
         osp = ctx.enter_context(tc.tile_pool(name="osp", bufs=4))
         ps4 = ctx.enter_context(tc.psum_pool(name="ps4", bufs=4))
@@ -49,13 +49,17 @@ def tile_dartslayer_kernel(tc, x, alphas, coeffs, out):
         out_view = out.rearrange("(r b) j -> r b j", b=NB)
 
         def load_chunk(view, c, label, pieces):
-            tl = acp.tile([P, PACK, JC * K], BF16, name=label, tag="ac")
             w = JC * K // pieces
+            tl = acp.tile([P, pieces, PACK, w], BF16, name=label, tag="ac")
             for h in range(pieces):
-                nc.sync.dma_start(
-                    out=tl[:, :, h * w : (h + 1) * w], in_=view[:, :, c * JC * K + h * w : c * JC * K + (h + 1) * w]
-                )
+                nc.sync.dma_start(out=tl[:, h], in_=view[:, :, c * JC * K + h * w : c * JC * K + (h + 1) * w])
             return tl
+
+        def columns(tl, pieces, j0, nj):
+            per = JC // pieces
+            h = j0 // per
+            assert (j0 + nj - 1) // per == h
+            return tl[:, h, :, (j0 - h * per) * K : (j0 - h * per + nj) * K]
 
         a_sb = [None] * NCH
         c_sb = [None] * NCH
@@ -66,10 +70,9 @@ def tile_dartslayer_kernel(tc, x, alphas, coeffs, out):
 
         a_sb[0] = load_chunk(a_view, 0, "a0", 2)
         a_sb[1] = load_chunk(a_view, 1, "a1", 2)
+        a_sb[2] = load_chunk(a_view, 2, "a2", 1)
         x_sb = k8.tile([P, XW], BF16, name="x_sb", tag="k8", align_bytes=64)
         nc.sync.dma_start(out=x_sb[:], in_=x_view)
-        a_sb[2] = load_chunk(a_view, 2, "a2", 1)
-        a_sb[3] = load_chunk(a_view, 3, "a3", 1)
 
         ident = const.tile([P, P], F32, name="ident")
         make_identity(nc, ident[:])
@@ -93,18 +96,26 @@ def tile_dartslayer_kernel(tc, x, alphas, coeffs, out):
         def new_e(c):
             e_sb[c] = big.tile([P, JC, PACK, K], F32, name="e%d" % c, tag="k16")
 
-        def a_by_j(c):
-            return a_sb[c][:].rearrange("p t (j k) -> p j t k", k=K)
+        PIECES = (2, 2, 1, 1)
 
-        def tree(c, j0, nj):
-            a6 = a_sb[c][:].rearrange("p t (j g h e) -> p g j t h e", g=2, h=2, e=2)[:, :, j0 : j0 + nj]
+        def a_by_j(c, j0, nj):
+            return columns(a_sb[c], PIECES[c], j0, nj).rearrange("p t (j k) -> p j t k", k=K)
+
+        def tree1(c, j0, nj):
+            a6 = columns(a_sb[c], PIECES[c], j0, nj).rearrange("p t (j g h e) -> p g j t h e", g=2, h=2, e=2)
             m1 = mt.tile([P, 2, nj, PACK, 2], BF16, name="m1")
             nc.vector.tensor_tensor(
                 out=m1[:].rearrange("p h j t e -> p j t h e"), in0=a6[:, 0], in1=a6[:, 1], op=ALU.max
             )
+            return m1
+
+        def tree2(m1, nj):
             m2 = mt.tile([P, nj, PACK, 2], BF16, name="m2")
             nc.vector.tensor_tensor(out=m2[:], in0=m1[:, 0], in1=m1[:, 1], op=ALU.max)
-            m3 = mt.tile([P, nj, PACK], BF16, name="m3", bufs=3)
+            return m2
+
+        def tree3(m2, nj):
+            m3 = mt.tile([P, nj, PACK], BF16, name="m3", bufs=4)
             nc.vector.tensor_tensor(out=m3[:], in0=m2[:, :, :, 0], in1=m2[:, :, :, 1], op=ALU.max)
             return m3
 
@@ -113,12 +124,12 @@ def tile_dartslayer_kernel(tc, x, alphas, coeffs, out):
 
         def sub_vector(c, m3, j0, nj, off):
             nc.vector.tensor_tensor(
-                out=e_sb[c][:, j0 : j0 + nj], in0=a_by_j(c)[:, j0 : j0 + nj], in1=spread(m3, off, nj), op=ALU.subtract
+                out=e_sb[c][:, j0 : j0 + nj], in0=a_by_j(c, j0, nj), in1=spread(m3, off, nj), op=ALU.subtract
             )
 
         def sub_exp_tensor(c, m3, j0, off):
             dps = psa.tile([P, TJ, PACK, K], F32, name="dps", tag="acc")
-            nc.tensor.matmul(out=dps[:], lhsT=ident_bf[:], rhs=a_by_j(c)[:, j0 : j0 + TJ], start=True, stop=False)
+            nc.tensor.matmul(out=dps[:], lhsT=ident_bf[:], rhs=a_by_j(c, j0, TJ), start=True, stop=False)
             nc.tensor.matmul(out=dps[:], lhsT=neg_bf[:], rhs=spread(m3, off, TJ), start=False, stop=True)
             nc.scalar.activation(out=e_sb[c][:, j0 : j0 + TJ], in_=dps[:], func=ACT.Exp)
 
@@ -143,7 +154,7 @@ def tile_dartslayer_kernel(tc, x, alphas, coeffs, out):
         def times_coeffs(c):
             tt[c] = big.tile([P, NPRIM, CW], F32, name="tt%d" % c, tag="k16")
             planes = tt[c][:].rearrange("p k (j t) -> p j t k", t=PACK)
-            c4 = c_sb[c][:].rearrange("p t (j k) -> p j t k", k=K)
+            c4 = columns(c_sb[c], 1, 0, JC).rearrange("p t (j k) -> p j t k", k=K)
             for lo, hi in ((1, 4), (4, K)):
                 nc.vector.tensor_tensor(
                     out=planes[:, :, :, lo - 1 : hi - 1], in0=e_sb[c][:, :, :, lo:hi], in1=c4[:, :, :, lo:hi], op=ALU.mult
@@ -155,21 +166,31 @@ def tile_dartslayer_kernel(tc, x, alphas, coeffs, out):
         def prim_tile(label):
             return k8.tile([P, XW], BF16, name=label, tag="k8", align_bytes=64)
 
+        QJ = JC // 4
         new_e(0)
-        for h in range(2):
-            m3 = tree(0, h * HALF, HALF)
-            for q in range(HALF // TJ):
-                sub_exp_tensor(0, m3, h * HALF + q * TJ, q * TJ)
-        c_sb[0] = load_chunk(c_view, 0, "c0", 1)
-
         new_e(1)
-        m3 = tree(1, 0, HALF)
-        sub_exp_tensor(1, m3, 0, 0)
-        sub_exp_tensor(1, m3, TJ, TJ)
-        sub_vector(1, m3, 2 * TJ, HALF - 2 * TJ, 2 * TJ)
-        m3 = tree(1, HALF, HALF)
-        sub_vector(1, m3, HALF, HALF, 0)
-        c_sb[1] = load_chunk(c_view, 1, "c1", 1)
+        m1_0a = tree1(0, 0, HALF)
+        m2_0a = tree2(m1_0a, HALF)
+        m1_0b = tree1(0, HALF, HALF)
+        m3_0a = tree3(m2_0a, HALF)
+        for q in range(HALF // TJ):
+            sub_exp_tensor(0, m3_0a, q * TJ, q * TJ)
+        m2_0b = tree2(m1_0b, HALF)
+        m1_1a = tree1(1, 0, HALF)
+        m3_0b = tree3(m2_0b, HALF)
+        for q in range(HALF // TJ):
+            sub_exp_tensor(0, m3_0b, HALF + q * TJ, q * TJ)
+        a_sb[3] = load_chunk(a_view, 3, "a3", 1)
+        m2_1a = tree2(m1_1a, HALF)
+        m1_1b = tree1(1, HALF, HALF)
+        m3_1a = tree3(m2_1a, HALF)
+        sub_exp_tensor(1, m3_1a, 0, 0)
+        sub_exp_tensor(1, m3_1a, TJ, TJ)
+        sub_exp_tensor(1, m3_1a, 2 * TJ, 2 * TJ)
+        m2_1b = tree2(m1_1b, HALF)
+        sub_vector(1, m3_1a, 3 * TJ, TJ, 3 * TJ)
+        exp_sbuf(1, 3 * TJ, TJ)
+        m3_1b = tree3(m2_1b, HALF)
 
         xw = x_sb[:].bitcast(F32).rearrange("p (b r u) -> p b u r", b=NB, u=2)
         xgw = xg[:].bitcast(F32).rearrange("p (b r u) -> p b r u", b=NB, u=2)
@@ -179,42 +200,67 @@ def tile_dartslayer_kernel(tc, x, alphas, coeffs, out):
                 for u in range(2):
                     nc.tensor.transpose(xt[:, b2, u, :], xw[:, 2 * h + b2, u, :], ident[:])
             nc.scalar.copy(out=xgw[:, 2 * h : 2 * h + 2, :, :], in_=xt[:].rearrange("p b u r -> p b r u"))
-
         sum_chunk(0)
-        exp_sbuf(1, 2 * TJ, JC - 2 * TJ)
-        sum_chunk(1)
 
         new_e(2)
-        m3 = tree(2, 0, JC)
-        sub_vector(2, m3, 0, JC, 0)
-        c_sb[2] = load_chunk(c_view, 2, "c2", 1)
+        m1_2 = tree1(2, 0, JC)
+        sub_vector(1, m3_1b, HALF, QJ, 0)
+        exp_sbuf(1, HALF, QJ)
+        m2_2 = tree2(m1_2, JC)
+        sub_vector(1, m3_1b, HALF + QJ, QJ, QJ)
+        exp_sbuf(1, HALF + QJ, QJ)
+        c_sb[0] = load_chunk(c_view, 0, "c0", 1)
+        sum_chunk(1)
+        m3_2 = tree3(m2_2, JC)
+        new_e(3)
+        m1_3 = tree1(3, 0, JC)
+        sub_vector(2, m3_2, 0, HALF, 0)
+        exp_sbuf(2, 0, HALF)
+        m2_3 = tree2(m1_3, JC)
+        sub_vector(2, m3_2, HALF, HALF, HALF)
+        c_sb[1] = load_chunk(c_view, 1, "c1", 1)
         p_exp = prim_tile("p_exp")
         nc.scalar.activation(out=p_exp[:], in_=xg[:], func=ACT.Exp)
-        exp_sbuf(2, 0, JC)
+        exp_sbuf(2, HALF, HALF)
+        p_sq = prim_tile("p_sq")
+        nc.scalar.activation(out=p_sq[:], in_=xg[:], func=ACT.Square)
         sum_chunk(2)
+        m3_3 = tree3(m2_3, JC)
 
-        new_e(3)
-        m3 = tree(3, 0, JC)
-        sub_vector(3, m3, 0, JC, 0)
-        c_sb[3] = load_chunk(c_view, 3, "c3", 1)
-        exp_sbuf(3, 0, JC)
-        sum_chunk(3)
-
+        XH = XW // 2
         n_i = big.tile([P, XW], I32, name="n_i", tag="k16")
-        nc.vector.tensor_scalar(out=n_i[:], in0=xg[:], scalar1=0.5 / math.pi, scalar2=None, op0=ALU.mult)
         y = big.tile([P, XW], F32, name="y", tag="k16")
-        nc.vector.scalar_tensor_tensor(out=y[:], in0=n_i[:], scalar=-2.0 * math.pi, in1=xg[:], op0=ALU.mult, op1=ALU.add)
+
+        def turns(h):
+            cols = slice(h * XH, (h + 1) * XH)
+            nc.vector.tensor_scalar(out=n_i[:, cols], in0=xg[:, cols], scalar1=0.5 / math.pi, scalar2=None, op0=ALU.mult)
+
+        def reduced(h):
+            cols = slice(h * XH, (h + 1) * XH)
+            nc.vector.scalar_tensor_tensor(
+                out=y[:, cols], in0=n_i[:, cols], scalar=-2.0 * math.pi, in1=xg[:, cols], op0=ALU.mult, op1=ALU.add
+            )
+
+        turns(0)
+        sub_vector(3, m3_3, 0, HALF, 0)
+        exp_sbuf(3, 0, HALF)
+        turns(1)
+        sub_vector(3, m3_3, HALF, HALF, HALF)
+        c_sb[2] = load_chunk(c_view, 2, "c2", 1)
+        exp_sbuf(3, HALF, HALF)
+        sum_chunk(3)
+        reduced(0)
+        reduced(1)
         p_sin = prim_tile("p_sin")
         nc.scalar.activation(out=p_sin[:], in_=y[:], func=ACT.Sin, bias=sin_bias[:], scale=sin_scale[:])
+        lnx = big.tile([P, XW], F32, name="lnx", tag="k16")
+        nc.scalar.activation(out=lnx[:], in_=xg[:], func=ACT.Ln)
 
-        p_sq = prim_tile("p_sq")
-        nc.vector.tensor_tensor(out=p_sq[:], in0=xg[:], in1=xg[:], op=ALU.mult)
         quant_prim(0, xg[:])
         quant_prim(3, p_exp[:])
         quant_prim(1, p_sq[:])
         times_coeffs(0)
-        lnx = big.tile([P, XW], F32, name="lnx", tag="k16")
-        nc.scalar.activation(out=lnx[:], in_=xg[:], func=ACT.Ln)
+        c_sb[3] = load_chunk(c_view, 3, "c3", 1)
         times_coeffs(1)
         quant_prim(6, p_sin[:])
 

@@ -32,9 +32,9 @@ def tile_dartslayer_kernel(tc, x, alphas, coeffs, out):
     nc = tc.nc
     with ExitStack() as ctx:
         const = ctx.enter_context(tc.tile_pool(name="const", bufs=1))
-        big = ctx.enter_context(tc.tile_pool(name="big", bufs=6))
+        big = ctx.enter_context(tc.tile_pool(name="big", bufs=1))
         acp = ctx.enter_context(tc.tile_pool(name="acp", bufs=3))
-        k8 = ctx.enter_context(tc.tile_pool(name="k8", bufs=4))
+        k8 = ctx.enter_context(tc.tile_pool(name="k8", bufs=1))
         keep = ctx.enter_context(tc.tile_pool(name="keep", bufs=1))
         mt = ctx.enter_context(tc.tile_pool(name="mt", bufs=2))
         wcp = ctx.enter_context(tc.tile_pool(name="wcp", bufs=2))
@@ -71,7 +71,7 @@ def tile_dartslayer_kernel(tc, x, alphas, coeffs, out):
         a_sb[0] = load_chunk(a_view, 0, "a0", 2)
         a_sb[1] = load_chunk(a_view, 1, "a1", 2)
         a_sb[2] = load_chunk(a_view, 2, "a2", 1)
-        x_sb = k8.tile([P, XW], BF16, name="x_sb", tag="k8", align_bytes=64)
+        x_sb = k8.tile([P, XW], BF16, name="x_sb", tag="h0", align_bytes=64)
         nc.sync.dma_start(out=x_sb[:], in_=x_view)
 
         ident = const.tile([P, P], F32, name="ident")
@@ -94,7 +94,7 @@ def tile_dartslayer_kernel(tc, x, alphas, coeffs, out):
         ps = keep.tile([P, NPRIM, NB * P], U8, name="ps", align_bytes=64)
 
         def new_e(c):
-            e_sb[c] = big.tile([P, JC, PACK, K], F32, name="e%d" % c, tag="k16")
+            e_sb[c] = big.tile([P, JC, PACK, K], F32, name="e%d" % c, tag="k%d" % c)
 
         PIECES = (2, 2, 1, 1)
 
@@ -152,7 +152,7 @@ def tile_dartslayer_kernel(tc, x, alphas, coeffs, out):
                     )
 
         def times_coeffs(c):
-            tt[c] = big.tile([P, NPRIM, CW], F32, name="tt%d" % c, tag="k16")
+            tt[c] = big.tile([P, NPRIM, CW], F32, name="tt%d" % c, tag="k%d" % ((c + 4) % 5))
             planes = tt[c][:].rearrange("p k (j t) -> p j t k", t=PACK)
             c4 = columns(c_sb[c], 1, 0, JC).rearrange("p t (j k) -> p j t k", k=K)
             for lo, hi in ((1, 4), (4, K)):
@@ -163,8 +163,8 @@ def tile_dartslayer_kernel(tc, x, alphas, coeffs, out):
         def quant_prim(k, src):
             nc.vector.quantize_mx(out=pc[:, k, :].bitcast(FP8X4), scales=ps[:, k, :], in_=src)
 
-        def prim_tile(label):
-            return k8.tile([P, XW], BF16, name=label, tag="k8", align_bytes=64)
+        def prim_tile(label, slot):
+            return k8.tile([P, XW], BF16, name=label, tag=slot, align_bytes=64)
 
         QJ = JC // 4
         new_e(0)
@@ -219,17 +219,15 @@ def tile_dartslayer_kernel(tc, x, alphas, coeffs, out):
         m2_3 = tree2(m1_3, JC)
         sub_vector(2, m3_2, HALF, HALF, HALF)
         c_sb[1] = load_chunk(c_view, 1, "c1", 1)
-        p_exp = prim_tile("p_exp")
+        p_exp = prim_tile("p_exp", "h1")
         nc.scalar.activation(out=p_exp[:], in_=xg[:], func=ACT.Exp)
         exp_sbuf(2, HALF, HALF)
-        p_sq = prim_tile("p_sq")
-        nc.scalar.activation(out=p_sq[:], in_=xg[:], func=ACT.Square)
         sum_chunk(2)
         m3_3 = tree3(m2_3, JC)
 
         XH = XW // 2
-        n_i = big.tile([P, XW], I32, name="n_i", tag="k16")
-        y = big.tile([P, XW], F32, name="y", tag="k16")
+        n_i = big.tile([P, XW], I32, name="n_i", tag="k4")
+        y = big.tile([P, XW], F32, name="y", tag="k5")
 
         def turns(h):
             cols = slice(h * XH, (h + 1) * XH)
@@ -251,20 +249,19 @@ def tile_dartslayer_kernel(tc, x, alphas, coeffs, out):
         sum_chunk(3)
         reduced(0)
         reduced(1)
-        p_sin = prim_tile("p_sin")
+        p_sin = prim_tile("p_sin", "h2")
         nc.scalar.activation(out=p_sin[:], in_=y[:], func=ACT.Sin, bias=sin_bias[:], scale=sin_scale[:])
-        lnx = big.tile([P, XW], F32, name="lnx", tag="k16")
+        lnx = big.tile([P, XW], F32, name="lnx", tag="k5")
         nc.scalar.activation(out=lnx[:], in_=xg[:], func=ACT.Ln)
 
         quant_prim(0, xg[:])
         quant_prim(3, p_exp[:])
-        quant_prim(1, p_sq[:])
         times_coeffs(0)
         c_sb[3] = load_chunk(c_view, 3, "c3", 1)
         times_coeffs(1)
         quant_prim(6, p_sin[:])
 
-        rt = k8.tile([P, NCH, CW], F32, name="rt", tag="k8", align_bytes=64)
+        rt = k8.tile([P, NCH, CW], F32, name="rt", tag="h0", align_bytes=64)
         for c in range(NCH):
             nc.scalar.activation(out=rt[:, c, :], in_=st[c][:].rearrange("p q n -> p (q n)"), func=ACT.Ln)
         rt_flat = rt[:].rearrange("p c n -> p (c n)")
@@ -274,16 +271,18 @@ def tile_dartslayer_kernel(tc, x, alphas, coeffs, out):
             for q in range(PACK):
                 nc.tensor.transpose(rr[c][:, q, :], rt[:, c, q * P : (q + 1) * P], ident[:])
 
-        p_rec = prim_tile("p_rec")
+        p_rec = prim_tile("p_rec", "h1")
         nc.scalar.activation(out=p_rec[:], in_=lnx[:], func=ACT.Exp, scale=-1.0)
-        p_cube = prim_tile("p_cube")
+        p_cube = prim_tile("p_cube", "h3")
         nc.scalar.activation(out=p_cube[:], in_=lnx[:], func=ACT.Exp, scale=3.0)
 
         times_coeffs(2)
-        p_ln = prim_tile("p_ln")
+        p_ln = prim_tile("p_ln", "h2")
         nc.vector.tensor_copy(out=p_ln[:], in_=lnx[:])
         times_coeffs(3)
         quant_prim(4, p_ln[:])
+        p_sq = prim_tile("p_sq", "h2")
+        nc.scalar.activation(out=p_sq[:], in_=xg[:], func=ACT.Square)
 
         wq = [None] * NCH
         wc = [None] * NCH
@@ -326,7 +325,7 @@ def tile_dartslayer_kernel(tc, x, alphas, coeffs, out):
                 nc.sync.dma_start(out=out_view[:, 4 * h : 4 * h + 4, c * JC : (c + 1) * JC], in_=ost[:])
 
         for c in range(NCH):
-            wq[c] = k8.tile([P, NPRIM, CW], BF16, name="wq", tag="k8", align_bytes=64)
+            wq[c] = k8.tile([P, NPRIM, CW], BF16, name="wq", tag=("h0", "h2", "h1", "h3")[c], align_bytes=64)
             wc[c] = wcp.tile([P, NPRIM * JC], U32, name="wc", align_bytes=64)
             ws[c] = wcp.tile([P, NPRIM * JC], U8, name="ws", align_bytes=64)
             scale_part(c, 0, LO)
@@ -338,4 +337,5 @@ def tile_dartslayer_kernel(tc, x, alphas, coeffs, out):
             quant_part(c, 6, 7)
             if c == 0:
                 quant_prim(2, p_cube[:])
+                quant_prim(1, p_sq[:])
             multiply_chunk(c)

@@ -82,12 +82,13 @@ def tile_dartslayer_kernel(tc, x, alphas, coeffs, out):
         nc.vector.tensor_scalar(out=neg_bf[:], in0=ident[:], scalar1=-1.0, scalar2=None, op0=ALU.mult)
         probe = const.tile([P, 1], F32, name="probe")
         nc.vector.memset(probe[:], 0.75)
-        probe_i = const.tile([P, 1], I32, name="probe_i")
-        nc.vector.tensor_copy(out=probe_i[:], in_=probe[:])
+        probe_u = const.tile([P, 1], U32, name="probe_u")
+        nc.scalar.activation(out=probe_u[:], in_=probe[:], func=ACT.Copy)
+        probe_i = probe_u[:].bitcast(I32)
         sin_scale = const.tile([P, 1], F32, name="sin_scale")
-        nc.vector.tensor_scalar(out=sin_scale[:], in0=probe_i[:], scalar1=2.0, scalar2=-1.0, op0=ALU.mult, op1=ALU.add)
+        nc.vector.tensor_scalar(out=sin_scale[:], in0=probe_i, scalar1=2.0, scalar2=-1.0, op0=ALU.mult, op1=ALU.add)
         sin_bias = const.tile([P, 1], F32, name="sin_bias")
-        nc.vector.tensor_scalar(out=sin_bias[:], in0=probe_i[:], scalar1=-math.pi, scalar2=math.pi, op0=ALU.mult, op1=ALU.add)
+        nc.vector.tensor_scalar(out=sin_bias[:], in0=probe_i, scalar1=-math.pi, scalar2=math.pi, op0=ALU.mult, op1=ALU.add)
 
         xg = keep.tile([P, XW], BF16, name="xg", align_bytes=64)
         pc = keep.tile([P, NPRIM, NB * P], U32, name="pc", align_bytes=64)
@@ -201,6 +202,8 @@ def tile_dartslayer_kernel(tc, x, alphas, coeffs, out):
                     nc.tensor.transpose(xt[:, b2, u, :], xw[:, 2 * h + b2, u, :], ident[:])
             nc.scalar.copy(out=xgw[:, 2 * h : 2 * h + 2, :, :], in_=xt[:].rearrange("p b u r -> p b r u"))
         sum_chunk(0)
+        n_u = big.tile([P, XW], U32, name="n_u", tag="k4")
+        nc.scalar.activation(out=n_u[:], in_=xg[:], func=ACT.Copy, scale=0.5 / math.pi)
 
         new_e(2)
         m1_2 = tree1(2, 0, JC)
@@ -226,23 +229,16 @@ def tile_dartslayer_kernel(tc, x, alphas, coeffs, out):
         m3_3 = tree3(m2_3, JC)
 
         XH = XW // 2
-        n_i = big.tile([P, XW], I32, name="n_i", tag="k4")
         y = big.tile([P, XW], F32, name="y", tag="k5")
-
-        def turns(h):
-            cols = slice(h * XH, (h + 1) * XH)
-            nc.vector.tensor_scalar(out=n_i[:, cols], in0=xg[:, cols], scalar1=0.5 / math.pi, scalar2=None, op0=ALU.mult)
 
         def reduced(h):
             cols = slice(h * XH, (h + 1) * XH)
             nc.vector.scalar_tensor_tensor(
-                out=y[:, cols], in0=n_i[:, cols], scalar=-2.0 * math.pi, in1=xg[:, cols], op0=ALU.mult, op1=ALU.add
+                out=y[:, cols], in0=n_u[:, cols].bitcast(I32), scalar=-2.0 * math.pi, in1=xg[:, cols], op0=ALU.mult, op1=ALU.add
             )
 
-        turns(0)
         sub_vector(3, m3_3, 0, HALF, 0)
         exp_sbuf(3, 0, HALF)
-        turns(1)
         sub_vector(3, m3_3, HALF, HALF, HALF)
         c_sb[2] = load_chunk(c_view, 2, "c2", 1)
         exp_sbuf(3, HALF, HALF)
@@ -255,7 +251,10 @@ def tile_dartslayer_kernel(tc, x, alphas, coeffs, out):
         nc.scalar.activation(out=lnx[:], in_=xg[:], func=ACT.Ln)
 
         quant_prim(0, xg[:])
+        p_sq = prim_tile("p_sq", "h3")
+        nc.vector.tensor_tensor(out=p_sq[:], in0=xg[:], in1=xg[:], op=ALU.mult)
         quant_prim(3, p_exp[:])
+        quant_prim(1, p_sq[:])
         times_coeffs(0)
         c_sb[3] = load_chunk(c_view, 3, "c3", 1)
         times_coeffs(1)
@@ -281,8 +280,6 @@ def tile_dartslayer_kernel(tc, x, alphas, coeffs, out):
         nc.vector.tensor_copy(out=p_ln[:], in_=lnx[:])
         times_coeffs(3)
         quant_prim(4, p_ln[:])
-        p_sq = prim_tile("p_sq", "h2")
-        nc.scalar.activation(out=p_sq[:], in_=xg[:], func=ACT.Square)
 
         wq = [None] * NCH
         wc = [None] * NCH
@@ -337,5 +334,4 @@ def tile_dartslayer_kernel(tc, x, alphas, coeffs, out):
             quant_part(c, 6, 7)
             if c == 0:
                 quant_prim(2, p_cube[:])
-                quant_prim(1, p_sq[:])
             multiply_chunk(c)

@@ -33,13 +33,10 @@ def tile_dartslayer_kernel(tc, x, alphas, coeffs, out):
     with ExitStack() as ctx:
         const = ctx.enter_context(tc.tile_pool(name="const", bufs=1))
         big = ctx.enter_context(tc.tile_pool(name="big", bufs=1))
-        acp = ctx.enter_context(tc.tile_pool(name="acp", bufs=3))
         k8 = ctx.enter_context(tc.tile_pool(name="k8", bufs=1))
         keep = ctx.enter_context(tc.tile_pool(name="keep", bufs=1))
         mt = ctx.enter_context(tc.tile_pool(name="mt", bufs=2))
-        wcp = ctx.enter_context(tc.tile_pool(name="wcp", bufs=2))
-        osp = ctx.enter_context(tc.tile_pool(name="osp", bufs=4))
-        ps4 = ctx.enter_context(tc.psum_pool(name="ps4", bufs=4))
+        pst = ctx.enter_context(tc.psum_pool(name="pst", bufs=4))
         psa = ctx.enter_context(tc.psum_pool(name="psa", bufs=4))
         ctx.enter_context(tc.manual_schedule())
 
@@ -48,30 +45,34 @@ def tile_dartslayer_kernel(tc, x, alphas, coeffs, out):
         x_view = x.rearrange("(r b) i -> r (b i)", b=NB)
         out_view = out.rearrange("(r b) j -> r b j", b=NB)
 
-        def load_chunk(view, c, label, pieces):
-            w = JC * K // pieces
-            tl = acp.tile([P, pieces, PACK, w], BF16, name=label, tag="ac")
-            for h in range(pieces):
-                nc.sync.dma_start(out=tl[:, h], in_=view[:, :, c * JC * K + h * w : c * JC * K + (h + 1) * w])
+        def piece(tl, start, end):
+            return tl[:, start * PACK * K : end * PACK * K].rearrange("p (t w) -> p t w", t=PACK)
+
+        def load_chunk(view, c, label, bounds):
+            tl = k8.tile([P, JC * PACK * K], BF16, name=label, tag="s%d" % c, align_bytes=64)
+            for start, end in zip(bounds, bounds[1:]):
+                nc.sync.dma_start(
+                    out=piece(tl, start, end), in_=view[:, :, (c * JC + start) * K : (c * JC + end) * K]
+                )
             return tl
 
-        def columns(tl, pieces, j0, nj):
-            per = JC // pieces
-            h = j0 // per
-            assert (j0 + nj - 1) // per == h
-            return tl[:, h, :, (j0 - h * per) * K : (j0 - h * per + nj) * K]
+        def columns(tl, bounds, j0, nj):
+            start, end = [(a, b) for a, b in zip(bounds, bounds[1:]) if a <= j0 and j0 + nj <= b][0]
+            return piece(tl, start, end)[:, :, (j0 - start) * K : (j0 - start + nj) * K]
 
         a_sb = [None] * NCH
         c_sb = [None] * NCH
-        e_sb = [None] * NCH
+        e_pair = [None] * (NCH // 2)
         st = [None] * NCH
-        rr = [None] * NCH
-        tt = [None] * NCH
+        rb = [None] * NCH
+        tt = [None] * (NCH // 2)
 
-        a_sb[0] = load_chunk(a_view, 0, "a0", 2)
-        a_sb[1] = load_chunk(a_view, 1, "a1", 2)
-        a_sb[2] = load_chunk(a_view, 2, "a2", 1)
-        x_sb = k8.tile([P, XW], BF16, name="x_sb", tag="h0", align_bytes=64)
+        QJ = JC // 4
+        WHOLE = (0, JC)
+        PIECES = ((0, QJ, HALF, JC), (0, HALF, JC), WHOLE, WHOLE)
+        for c in range(NCH):
+            a_sb[c] = load_chunk(a_view, c, "a%d" % c, PIECES[c])
+        x_sb = k8.tile([P, XW], BF16, name="x_sb", tag="s4", align_bytes=64)
         nc.sync.dma_start(out=x_sb[:], in_=x_view)
 
         ident = const.tile([P, P], F32, name="ident")
@@ -80,24 +81,20 @@ def tile_dartslayer_kernel(tc, x, alphas, coeffs, out):
         nc.vector.tensor_copy(out=ident_bf[:], in_=ident[:])
         neg_bf = const.tile([P, P], BF16, name="neg_bf")
         nc.vector.tensor_scalar(out=neg_bf[:], in0=ident[:], scalar1=-1.0, scalar2=None, op0=ALU.mult)
-        probe = const.tile([P, 1], F32, name="probe")
-        nc.vector.memset(probe[:], 0.75)
-        probe_u = const.tile([P, 1], U32, name="probe_u")
-        nc.scalar.activation(out=probe_u[:], in_=probe[:], func=ACT.Copy)
-        probe_i = probe_u[:].bitcast(I32)
-        sin_scale = const.tile([P, 1], F32, name="sin_scale")
-        nc.vector.tensor_scalar(out=sin_scale[:], in0=probe_i, scalar1=2.0, scalar2=-1.0, op0=ALU.mult, op1=ALU.add)
-        sin_bias = const.tile([P, 1], F32, name="sin_bias")
-        nc.vector.tensor_scalar(out=sin_bias[:], in0=probe_i, scalar1=-math.pi, scalar2=math.pi, op0=ALU.mult, op1=ALU.add)
+        warm = const.tile([P, 1], F32, name="warm")
+        nc.scalar.activation(out=warm[:], in_=ident[:, 0:1], func=ACT.Exp)
 
         xg = keep.tile([P, XW], BF16, name="xg", align_bytes=64)
-        pc = keep.tile([P, NPRIM, NB * P], U32, name="pc", align_bytes=64)
         ps = keep.tile([P, NPRIM, NB * P], U8, name="ps", align_bytes=64)
+        wc = keep.tile([P, NPRIM, J], U32, name="wc", align_bytes=64)
+        ws = keep.tile([P, NPRIM, J], U8, name="ws", align_bytes=64)
 
-        def new_e(c):
-            e_sb[c] = big.tile([P, JC, PACK, K], F32, name="e%d" % c, tag="k%d" % c)
+        def new_e(pair):
+            e_pair[pair] = big.tile([P, 2 * JC, PACK, K], F32, name="e%d" % pair, tag="e%d" % pair, align_bytes=64)
 
-        PIECES = (2, 2, 1, 1)
+        def e_part(c, j0, nj):
+            first = (c % 2) * JC + j0
+            return e_pair[c // 2][:, first : first + nj]
 
         def a_by_j(c, j0, nj):
             return columns(a_sb[c], PIECES[c], j0, nj).rearrange("p t (j k) -> p j t k", k=K)
@@ -123,24 +120,25 @@ def tile_dartslayer_kernel(tc, x, alphas, coeffs, out):
         def spread(m3, off, nj):
             return m3[:, off : off + nj, :].unsqueeze(3).to_broadcast([P, nj, PACK, K])
 
-        def sub_vector(c, m3, j0, nj, off):
+        def exp_sbuf(c, j0, nj):
+            flat = e_part(c, j0, nj).rearrange("p j t k -> p (j t k)")
+            nc.scalar.activation(out=flat, in_=flat, func=ACT.Exp)
+
+        def sub_exp_vector(c, m3, j0, nj, off):
             nc.vector.tensor_tensor(
-                out=e_sb[c][:, j0 : j0 + nj], in0=a_by_j(c, j0, nj), in1=spread(m3, off, nj), op=ALU.subtract
+                out=e_part(c, j0, nj), in0=a_by_j(c, j0, nj), in1=spread(m3, off, nj), op=ALU.subtract
             )
+            exp_sbuf(c, j0, nj)
 
         def sub_exp_tensor(c, m3, j0, off):
             dps = psa.tile([P, TJ, PACK, K], F32, name="dps", tag="acc")
             nc.tensor.matmul(out=dps[:], lhsT=ident_bf[:], rhs=a_by_j(c, j0, TJ), start=True, stop=False)
             nc.tensor.matmul(out=dps[:], lhsT=neg_bf[:], rhs=spread(m3, off, TJ), start=False, stop=True)
-            nc.scalar.activation(out=e_sb[c][:, j0 : j0 + TJ], in_=dps[:], func=ACT.Exp)
-
-        def exp_sbuf(c, j0, nj):
-            flat = e_sb[c][:, j0 : j0 + nj].rearrange("p j t k -> p (j t k)")
-            nc.scalar.activation(out=flat, in_=flat, func=ACT.Exp)
+            nc.scalar.activation(out=e_part(c, j0, TJ), in_=dps[:], func=ACT.Exp)
 
         def sum_chunk(c):
-            e2 = e_sb[c][:].rearrange("p j t k -> p (j t) k")
-            st[c] = ps4.tile([P, PACK, P], F32, name="st", tag="t4")
+            e2 = e_part(c, 0, JC).rearrange("p j t k -> p (j t) k")
+            st[c] = pst.tile([P, PACK, P], F32, name="st", tag="t4")
             for q in range(PACK):
                 for k in range(K):
                     nc.tensor.matmul(
@@ -153,12 +151,12 @@ def tile_dartslayer_kernel(tc, x, alphas, coeffs, out):
                     )
 
         def times_coeffs(c):
-            tt[c] = big.tile([P, NPRIM, CW], F32, name="tt%d" % c, tag="k%d" % ((c + 4) % 5))
-            planes = tt[c][:].rearrange("p k (j t) -> p j t k", t=PACK)
-            c4 = columns(c_sb[c], 1, 0, JC).rearrange("p t (j k) -> p j t k", k=K)
+            planes = tt[c // 2][:, :, (c % 2) * CW : (c % 2 + 1) * CW].rearrange("p k (j t) -> p j t k", t=PACK)
+            e4 = e_part(c, 0, JC)
+            c4 = columns(c_sb[c], WHOLE, 0, JC).rearrange("p t (j k) -> p j t k", k=K)
             for lo, hi in ((1, 4), (4, K)):
                 nc.vector.tensor_tensor(
-                    out=planes[:, :, :, lo - 1 : hi - 1], in0=e_sb[c][:, :, :, lo:hi], in1=c4[:, :, :, lo:hi], op=ALU.mult
+                    out=planes[:, :, :, lo - 1 : hi - 1], in0=e4[:, :, :, lo:hi], in1=c4[:, :, :, lo:hi], op=ALU.mult
                 )
 
         def quant_prim(k, src):
@@ -167,171 +165,180 @@ def tile_dartslayer_kernel(tc, x, alphas, coeffs, out):
         def prim_tile(label, slot):
             return k8.tile([P, XW], BF16, name=label, tag=slot, align_bytes=64)
 
-        QJ = JC // 4
         new_e(0)
-        new_e(1)
-        m1_0a = tree1(0, 0, HALF)
-        m2_0a = tree2(m1_0a, HALF)
-        m1_0b = tree1(0, HALF, HALF)
-        m3_0a = tree3(m2_0a, HALF)
-        for q in range(HALF // TJ):
-            sub_exp_tensor(0, m3_0a, q * TJ, q * TJ)
-        m2_0b = tree2(m1_0b, HALF)
-        m1_1a = tree1(1, 0, HALF)
-        m3_0b = tree3(m2_0b, HALF)
-        for q in range(HALF // TJ):
-            sub_exp_tensor(0, m3_0b, HALF + q * TJ, q * TJ)
-        a_sb[3] = load_chunk(a_view, 3, "a3", 1)
-        m2_1a = tree2(m1_1a, HALF)
+        todo = [(0, start, end - start) for start, end in zip(PIECES[0], PIECES[0][1:])] + [(1, 0, HALF)]
+        m2 = tree2(tree1(*todo[0]), todo[0][2])
+        for this, following in zip(todo, todo[1:]):
+            m1_next = tree1(*following)
+            m3 = tree3(m2, this[2])
+            for q in range(this[2] // TJ):
+                sub_exp_tensor(0, m3, this[1] + q * TJ, q * TJ)
+            m2 = tree2(m1_next, following[2])
+        m2_1a = m2
+        c_sb[0] = load_chunk(c_view, 0, "c0", WHOLE)
         m1_1b = tree1(1, HALF, HALF)
         m3_1a = tree3(m2_1a, HALF)
-        sub_exp_tensor(1, m3_1a, 0, 0)
-        sub_exp_tensor(1, m3_1a, TJ, TJ)
-        sub_exp_tensor(1, m3_1a, 2 * TJ, 2 * TJ)
+        for q in range(3):
+            sub_exp_tensor(1, m3_1a, q * TJ, q * TJ)
+        sum_chunk(0)
         m2_1b = tree2(m1_1b, HALF)
-        sub_vector(1, m3_1a, 3 * TJ, TJ, 3 * TJ)
-        exp_sbuf(1, 3 * TJ, TJ)
+        sub_exp_vector(1, m3_1a, 3 * TJ, TJ, 3 * TJ)
         m3_1b = tree3(m2_1b, HALF)
+        new_e(1)
+        m1_2 = tree1(2, 0, JC)
+        sub_exp_vector(1, m3_1b, HALF, QJ, 0)
+        m2_2 = tree2(m1_2, JC)
+        sub_exp_vector(1, m3_1b, HALF + QJ, QJ, QJ)
+        c_sb[1] = load_chunk(c_view, 1, "c1", WHOLE)
 
         xw = x_sb[:].bitcast(F32).rearrange("p (b r u) -> p b u r", b=NB, u=2)
         xgw = xg[:].bitcast(F32).rearrange("p (b r u) -> p b r u", b=NB, u=2)
         for h in range(NB // 2):
-            xt = ps4.tile([P, 2, 2, P], F32, name="xt", tag="t4")
+            xt = psa.tile([P, 2, 2, P], F32, name="xt", tag="acc")
             for b2 in range(2):
                 for u in range(2):
                     nc.tensor.transpose(xt[:, b2, u, :], xw[:, 2 * h + b2, u, :], ident[:])
             nc.scalar.copy(out=xgw[:, 2 * h : 2 * h + 2, :, :], in_=xt[:].rearrange("p b u r -> p b r u"))
-        sum_chunk(0)
-        n_u = big.tile([P, XW], U32, name="n_u", tag="k4")
+        n_u = big.tile([P, XW], U32, name="n_u", tag="n", align_bytes=64)
         nc.scalar.activation(out=n_u[:], in_=xg[:], func=ACT.Copy, scale=0.5 / math.pi)
-
-        new_e(2)
-        m1_2 = tree1(2, 0, JC)
-        sub_vector(1, m3_1b, HALF, QJ, 0)
-        exp_sbuf(1, HALF, QJ)
-        m2_2 = tree2(m1_2, JC)
-        sub_vector(1, m3_1b, HALF + QJ, QJ, QJ)
-        exp_sbuf(1, HALF + QJ, QJ)
-        c_sb[0] = load_chunk(c_view, 0, "c0", 1)
         sum_chunk(1)
+
         m3_2 = tree3(m2_2, JC)
-        new_e(3)
         m1_3 = tree1(3, 0, JC)
-        sub_vector(2, m3_2, 0, HALF, 0)
-        exp_sbuf(2, 0, HALF)
+        sub_exp_vector(2, m3_2, 0, HALF, 0)
         m2_3 = tree2(m1_3, JC)
-        sub_vector(2, m3_2, HALF, HALF, HALF)
-        c_sb[1] = load_chunk(c_view, 1, "c1", 1)
-        p_exp = prim_tile("p_exp", "h1")
-        nc.scalar.activation(out=p_exp[:], in_=xg[:], func=ACT.Exp)
-        exp_sbuf(2, HALF, HALF)
+        sub_exp_vector(2, m3_2, HALF, HALF, HALF)
+        c_sb[2] = load_chunk(c_view, 2, "c2", WHOLE)
         sum_chunk(2)
         m3_3 = tree3(m2_3, JC)
-
-        XH = XW // 2
-        y = big.tile([P, XW], F32, name="y", tag="k5")
-
-        def reduced(h):
-            cols = slice(h * XH, (h + 1) * XH)
-            nc.vector.scalar_tensor_tensor(
-                out=y[:, cols], in0=n_u[:, cols].bitcast(I32), scalar=-2.0 * math.pi, in1=xg[:, cols], op0=ALU.mult, op1=ALU.add
-            )
-
-        sub_vector(3, m3_3, 0, HALF, 0)
-        exp_sbuf(3, 0, HALF)
-        sub_vector(3, m3_3, HALF, HALF, HALF)
-        c_sb[2] = load_chunk(c_view, 2, "c2", 1)
-        exp_sbuf(3, HALF, HALF)
+        sub_exp_vector(3, m3_3, 0, HALF, 0)
+        sub_exp_vector(3, m3_3, HALF, QJ, HALF)
+        sub_exp_vector(3, m3_3, HALF + QJ, QJ, HALF + QJ)
+        c_sb[3] = load_chunk(c_view, 3, "c3", WHOLE)
         sum_chunk(3)
-        reduced(0)
-        reduced(1)
-        p_sin = prim_tile("p_sin", "h2")
-        nc.scalar.activation(out=p_sin[:], in_=y[:], func=ACT.Sin, bias=sin_bias[:], scale=sin_scale[:])
-        lnx = big.tile([P, XW], F32, name="lnx", tag="k5")
+
+        lnx = big.tile([P, XW], F32, name="lnx", tag="l", align_bytes=64)
         nc.scalar.activation(out=lnx[:], in_=xg[:], func=ACT.Ln)
-
-        quant_prim(0, xg[:])
-        p_sq = prim_tile("p_sq", "h3")
-        nc.vector.tensor_tensor(out=p_sq[:], in0=xg[:], in1=xg[:], op=ALU.mult)
-        quant_prim(3, p_exp[:])
-        quant_prim(1, p_sq[:])
+        p_ln = prim_tile("p_ln", "s5")
+        nc.scalar.activation(out=p_ln[:], in_=xg[:], func=ACT.Ln)
+        tt[0] = big.tile([P, NPRIM, 2 * CW], F32, name="tt0", tag="t0", align_bytes=64)
         times_coeffs(0)
-        c_sb[3] = load_chunk(c_view, 3, "c3", 1)
-        times_coeffs(1)
-        quant_prim(6, p_sin[:])
-
-        rt = k8.tile([P, NCH, CW], F32, name="rt", tag="h0", align_bytes=64)
+        rt = k8.tile([P, NCH, CW], F32, name="rt", tag="s4", align_bytes=64)
         for c in range(NCH):
             nc.scalar.activation(out=rt[:, c, :], in_=st[c][:].rearrange("p q n -> p (q n)"), func=ACT.Ln)
-        rt_flat = rt[:].rearrange("p c n -> p (c n)")
-        nc.scalar.activation(out=rt_flat, in_=rt_flat, func=ACT.Exp, scale=-1.0)
-        for c in range(NCH):
-            rr[c] = ps4.tile([P, PACK, P], F32, name="rr", tag="t4")
+            rb[c] = psa.tile([P, PACK, P], F32, name="rb", tag="acc")
             for q in range(PACK):
-                nc.tensor.transpose(rr[c][:, q, :], rt[:, c, q * P : (q + 1) * P], ident[:])
-
-        p_rec = prim_tile("p_rec", "h1")
-        nc.scalar.activation(out=p_rec[:], in_=lnx[:], func=ACT.Exp, scale=-1.0)
-        p_cube = prim_tile("p_cube", "h3")
-        nc.scalar.activation(out=p_cube[:], in_=lnx[:], func=ACT.Exp, scale=3.0)
-
+                nc.tensor.transpose(rb[c][:, q, :], rt[:, c, q * P : (q + 1) * P], ident[:])
+        times_coeffs(1)
+        tt[1] = big.tile([P, NPRIM, 2 * CW], F32, name="tt1", tag="e0", align_bytes=64)
         times_coeffs(2)
-        p_ln = prim_tile("p_ln", "h2")
-        nc.vector.tensor_copy(out=p_ln[:], in_=lnx[:])
+        rr = k8.tile([P, NCH, CW], F32, name="rr", tag="s6", align_bytes=64)
+        for c in range(NCH):
+            nc.scalar.activation(out=rr[:, c, :], in_=rb[c][:].rearrange("p q n -> p (q n)"), func=ACT.Exp, scale=-1.0)
         times_coeffs(3)
+        y = n_u[:].bitcast(F32)
+        nc.vector.scalar_tensor_tensor(
+            out=y, in0=n_u[:].bitcast(I32), scalar=-2.0 * math.pi, in1=xg[:], op0=ALU.mult, op1=ALU.add
+        )
+        pc = big.tile([P, NPRIM, NB * P], U32, name="pc", tag="e1", align_bytes=64)
+        quant_prim(0, xg[:])
         quant_prim(4, p_ln[:])
 
-        wq = [None] * NCH
-        wc = [None] * NCH
-        ws = [None] * NCH
-        LO = 4
+        acc = []
+        for b in range(NB):
+            if b < 4:
+                acc.append(psa.tile([P, J], F32, name="acc%d" % b, tag="acc"))
+            else:
+                acc.append(pst.tile([P, J], F32, name="acc%d" % b, tag="t4"))
 
-        def scale_part(c, lo, hi):
-            nc.vector.tensor_tensor(
-                out=wq[c][:, lo:hi, :],
-                in0=tt[c][:, lo:hi, :],
-                in1=rr[c][:].rearrange("p q n -> p (q n)").unsqueeze(1).to_broadcast([P, hi - lo, CW]),
-                op=ALU.mult,
-            )
+        def scaled_tile(planes, slot):
+            return k8.tile([P, planes, NCH * CW], BF16, name="wq", tag=slot, align_bytes=64)
 
-        def quant_part(c, lo, hi):
-            flat = wq[c][:].rearrange("p k n -> p (k n)")
+        def scale_planes(wq, at, lo, hi):
+            for pair in range(NCH // 2):
+                inv = rr[:, 2 * pair : 2 * pair + 2, :].rearrange("p c n -> p (c n)")
+                nc.vector.tensor_tensor(
+                    out=wq[:, at : at + hi - lo, 2 * pair * CW : 2 * (pair + 1) * CW],
+                    in0=tt[pair][:, lo:hi, :],
+                    in1=inv.unsqueeze(1).to_broadcast([P, hi - lo, 2 * CW]),
+                    op=ALU.mult,
+                )
+
+        def quant_planes(wq, at, lo, hi):
             nc.vector.quantize_mx(
-                out=wc[c][:, lo * JC : hi * JC].bitcast(FP8X4),
-                scales=ws[c][:, lo * JC : hi * JC],
-                in_=flat[:, lo * CW : hi * CW],
+                out=wc[:, lo:hi, :].rearrange("p k n -> p (k n)").bitcast(FP8X4),
+                scales=ws[:, lo:hi, :].rearrange("p k n -> p (k n)"),
+                in_=wq[:, at : at + hi - lo, :].rearrange("p k n -> p (k n)"),
             )
 
-        def multiply_chunk(c):
-            for h in range(2):
-                acc = psa.tile([P, 4, JC], F32, name="acc", tag="acc")
-                for b4 in range(4):
-                    bt = 4 * h + b4
-                    for k in range(NPRIM):
-                        nc.tensor.matmul_mx(
-                            out=acc[:, b4, :],
-                            lhsT=pc[:, k, bt * P : (bt + 1) * P].bitcast(FP8X4),
-                            lhsT_scale=ps[:, k, bt * P : (bt + 1) * P],
-                            rhs=wc[c][:, k * JC : (k + 1) * JC].bitcast(FP8X4),
-                            rhs_scale=ws[c][:, k * JC : (k + 1) * JC],
-                            start=(k == 0),
-                            stop=(k == NPRIM - 1),
-                        )
-                ost = osp.tile([P, 4, JC], F32, name="ost")
-                nc.scalar.copy(out=ost[:], in_=acc[:])
-                nc.sync.dma_start(out=out_view[:, 4 * h : 4 * h + 4, c * JC : (c + 1) * JC], in_=ost[:])
+        FIRST, LAST = 4, 6
 
-        for c in range(NCH):
-            wq[c] = k8.tile([P, NPRIM, CW], BF16, name="wq", tag=("h0", "h2", "h1", "h3")[c], align_bytes=64)
-            wc[c] = wcp.tile([P, NPRIM * JC], U32, name="wc", align_bytes=64)
-            ws[c] = wcp.tile([P, NPRIM * JC], U8, name="ws", align_bytes=64)
-            scale_part(c, 0, LO)
-            scale_part(c, LO, NPRIM)
-            quant_part(c, 0, 4)
-            if c == 0:
-                quant_prim(5, p_rec[:])
-            quant_part(c, 4, 6)
-            quant_part(c, 6, 7)
-            if c == 0:
-                quant_prim(2, p_cube[:])
-            multiply_chunk(c)
+        def multiply(k, blocks=range(NB)):
+            for b in blocks:
+                nc.tensor.matmul_mx(
+                    out=acc[b][:],
+                    lhsT=pc[:, k, b * P : (b + 1) * P].bitcast(FP8X4),
+                    lhsT_scale=ps[:, k, b * P : (b + 1) * P],
+                    rhs=wc[:, k, :].bitcast(FP8X4),
+                    rhs_scale=ws[:, k, :],
+                    start=(k == FIRST),
+                    stop=(k == LAST),
+                )
+
+        def quant_rows(k, src, half):
+            words = slice(half * NB * P // 2, (half + 1) * NB * P // 2)
+            cols = slice(half * XW // 2, (half + 1) * XW // 2)
+            nc.vector.quantize_mx(out=pc[:, k, words].bitcast(FP8X4), scales=ps[:, k, words], in_=src[:, cols])
+
+        p_exp = prim_tile("p_exp", "s4")
+        nc.scalar.activation(out=p_exp[:], in_=xg[:], func=ACT.Exp)
+        p_cube = prim_tile("p_cube", "s5")
+        nc.scalar.activation(out=p_cube[:], in_=lnx[:], func=ACT.Exp, scale=3.0)
+        wq_a = scaled_tile(2, "s0")
+        scale_planes(wq_a, 0, 3, 5)
+        wq_b = scaled_tile(2, "s1")
+        scale_planes(wq_b, 0, 0, 1)
+        quant_planes(wq_a, 0, 3, 5)
+        multiply(4)
+        quant_prim(3, p_exp[:])
+        multiply(3)
+        p_rec = prim_tile("p_rec", "s4")
+        nc.scalar.activation(out=p_rec[:], in_=lnx[:], func=ACT.Exp, scale=-1.0)
+        p_sq = prim_tile("p_sq", "s0")
+        nc.scalar.activation(out=p_sq[:], in_=xg[:], func=ACT.Square)
+        wq_c = scaled_tile(2, "s2")
+        scale_planes(wq_c, 1, 2, 3)
+        quant_planes(wq_b, 0, 0, 1)
+        multiply(0)
+        scale_planes(wq_c, 0, 1, 2)
+        quant_planes(wq_c, 1, 2, 3)
+        quant_prim(2, p_cube[:])
+        multiply(2)
+        p_sin = prim_tile("p_sin", "s5")
+        for i in range(2):
+            cols = slice(i * XW // 2, (i + 1) * XW // 2)
+            nc.scalar.activation(out=p_sin[:, cols], in_=y[:, cols], func=ACT.Sin)
+        wq_d = scaled_tile(2, "s3")
+        scale_planes(wq_d, 0, 5, 6)
+        quant_planes(wq_c, 0, 1, 2)
+        quant_rows(1, p_sq, 0)
+        multiply(1, range(4))
+        quant_planes(wq_d, 0, 5, 6)
+        scale_planes(wq_d, 1, 6, 7)
+        quant_rows(5, p_rec, 0)
+        multiply(5, range(4))
+        quant_planes(wq_d, 1, 6, 7)
+        quant_rows(6, p_sin, 0)
+        multiply(6, range(4))
+        quant_rows(1, p_sq, 1)
+        multiply(1, range(4, NB))
+        quant_rows(5, p_rec, 1)
+        quant_rows(6, p_sin, 1)
+        for pair in ((4, 5), (6, 7)):
+            multiply(5, pair)
+            multiply(6, pair)
+        ost = big.tile([P, NB, J], F32, name="ost", tag="l", align_bytes=64)
+        for b in range(0, NB, 2):
+            nc.scalar.copy(out=ost[:, b, :], in_=acc[b][:])
+            nc.vector.tensor_copy(out=ost[:, b + 1, :], in_=acc[b + 1][:])
+            nc.sync.dma_start(out=out_view[:, b : b + 2, :], in_=ost[:, b : b + 2, :])

@@ -254,8 +254,8 @@ def tile_dartslayer_kernel(tc, x, alphas, coeffs, out):
         def scaled_tile(planes, slot):
             return k8.tile([P, planes, NCH * CW], BF16, name="wq", tag=slot, align_bytes=64)
 
-        def scale_planes(wq, at, lo, hi):
-            for pair in range(NCH // 2):
+        def scale_planes(wq, at, lo, hi, pairs=range(NCH // 2)):
+            for pair in pairs:
                 inv = rr[:, 2 * pair : 2 * pair + 2, :].rearrange("p c n -> p (c n)")
                 nc.vector.tensor_tensor(
                     out=wq[:, at : at + hi - lo, 2 * pair * CW : 2 * (pair + 1) * CW],
@@ -302,36 +302,41 @@ def tile_dartslayer_kernel(tc, x, alphas, coeffs, out):
         multiply(4)
         quant_prim(3, p_exp[:])
         multiply(3)
-        p_rec = prim_tile("p_rec", "s4")
+        p_rec = prim_tile("p_rec", "s3")
         nc.scalar.activation(out=p_rec[:], in_=lnx[:], func=ACT.Exp, scale=-1.0)
         p_sq = prim_tile("p_sq", "s0")
         nc.scalar.activation(out=p_sq[:], in_=xg[:], func=ACT.Square)
+        p_sin = prim_tile("p_sin", "s1")
+        ROWS = (range(4), range(4, NB))
+
+        def rows_of(k, src, half):
+            quant_rows(k, src, half)
+            multiply(k, ROWS[half])
+
         wq_c = scaled_tile(2, "s2")
         scale_planes(wq_c, 1, 2, 3)
         quant_planes(wq_b, 0, 0, 1)
         multiply(0)
-        scale_planes(wq_c, 0, 1, 2)
-        quant_planes(wq_c, 1, 2, 3)
-        quant_prim(2, p_cube[:])
-        multiply(2)
-        p_sin = prim_tile("p_sin", "s5")
         for i in range(2):
             cols = slice(i * XW // 2, (i + 1) * XW // 2)
             nc.scalar.activation(out=p_sin[:, cols], in_=y[:, cols], func=ACT.Sin)
-        wq_d = scaled_tile(2, "s3")
-        scale_planes(wq_d, 0, 5, 6)
+        scale_planes(wq_c, 0, 1, 2, (0,))
+        quant_planes(wq_c, 1, 2, 3)
+        scale_planes(wq_c, 0, 1, 2, (1,))
+        rows_of(2, p_cube, 0)
+        wq_d = scaled_tile(2, "s4")
+        scale_planes(wq_d, 0, 5, 6, (0,))
         quant_planes(wq_c, 0, 1, 2)
-        quant_rows(1, p_sq, 0)
-        multiply(1, range(4))
+        rows_of(2, p_cube, 1)
+        scale_planes(wq_d, 0, 5, 6, (1,))
+        rows_of(1, p_sq, 0)
         quant_planes(wq_d, 0, 5, 6)
-        scale_planes(wq_d, 1, 6, 7)
-        quant_rows(5, p_rec, 0)
-        multiply(5, range(4))
+        scale_planes(wq_d, 1, 6, 7, (0,))
+        rows_of(5, p_rec, 0)
+        scale_planes(wq_d, 1, 6, 7, (1,))
+        rows_of(1, p_sq, 1)
         quant_planes(wq_d, 1, 6, 7)
-        quant_rows(6, p_sin, 0)
-        multiply(6, range(4))
-        quant_rows(1, p_sq, 1)
-        multiply(1, range(4, NB))
+        rows_of(6, p_sin, 0)
         quant_rows(5, p_rec, 1)
         quant_rows(6, p_sin, 1)
         for pair in ((4, 5), (6, 7)):

@@ -180,7 +180,6 @@ def tile_dartslayer_kernel(tc, x, alphas, coeffs, out):
         m3_1a = tree3(m2_1a, HALF)
         for q in range(3):
             sub_exp_tensor(1, m3_1a, q * TJ, q * TJ)
-        sum_chunk(0)
         m2_1b = tree2(m1_1b, HALF)
         sub_exp_vector(1, m3_1a, 3 * TJ, TJ, 3 * TJ)
         m3_1b = tree3(m2_1b, HALF)
@@ -201,6 +200,7 @@ def tile_dartslayer_kernel(tc, x, alphas, coeffs, out):
             nc.scalar.copy(out=xgw[:, 2 * h : 2 * h + 2, :, :], in_=xt[:].rearrange("p b u r -> p b r u"))
         n_u = big.tile([P, XW], U32, name="n_u", tag="n", align_bytes=64)
         nc.scalar.activation(out=n_u[:], in_=xg[:], func=ACT.Copy, scale=0.5 / math.pi)
+        sum_chunk(0)
         sum_chunk(1)
 
         m3_2 = tree3(m2_2, JC)

@@ -65,7 +65,8 @@ def tile_dartslayer_kernel(tc, x, alphas, coeffs, out):
         e_pair = [None] * (NCH // 2)
         st = [None] * NCH
         rb = [None] * NCH
-        tt = [None] * (NCH // 2)
+        tt_planes = [None] * (NCH // 2)
+        tt_pairs = [None] * (NCH // 2)
 
         QJ = JC // 4
         WHOLE = (0, JC)
@@ -100,16 +101,14 @@ def tile_dartslayer_kernel(tc, x, alphas, coeffs, out):
             return columns(a_sb[c], PIECES[c], j0, nj).rearrange("p t (j k) -> p j t k", k=K)
 
         def tree1(c, j0, nj):
-            a6 = columns(a_sb[c], PIECES[c], j0, nj).rearrange("p t (j g h e) -> p g j t h e", g=2, h=2, e=2)
-            m1 = mt.tile([P, 2, nj, PACK, 2], BF16, name="m1")
-            nc.vector.tensor_tensor(
-                out=m1[:].rearrange("p h j t e -> p j t h e"), in0=a6[:, 0], in1=a6[:, 1], op=ALU.max
-            )
+            a6 = columns(a_sb[c], PIECES[c], j0, nj).rearrange("p t (j g f) -> p g j t f", g=2, f=4)
+            m1 = mt.tile([P, nj, PACK, 4], BF16, name="m1")
+            nc.vector.tensor_tensor(out=m1[:], in0=a6[:, 0], in1=a6[:, 1], op=ALU.max)
             return m1
 
         def tree2(m1, nj):
             m2 = mt.tile([P, nj, PACK, 2], BF16, name="m2")
-            nc.vector.tensor_tensor(out=m2[:], in0=m1[:, 0], in1=m1[:, 1], op=ALU.max)
+            nc.vector.tensor_tensor(out=m2[:], in0=m1[:, :, :, 0:2], in1=m1[:, :, :, 2:4], op=ALU.max)
             return m2
 
         def tree3(m2, nj):
@@ -151,13 +150,32 @@ def tile_dartslayer_kernel(tc, x, alphas, coeffs, out):
                     )
 
         def times_coeffs(c):
-            planes = tt[c // 2][:, :, (c % 2) * CW : (c % 2 + 1) * CW].rearrange("p k (j t) -> p j t k", t=PACK)
+            first = (c % 2) * CW
             e4 = e_part(c, 0, JC)
             c4 = columns(c_sb[c], WHOLE, 0, JC).rearrange("p t (j k) -> p j t k", k=K)
-            for lo, hi in ((1, 4), (4, K)):
-                nc.vector.tensor_tensor(
-                    out=planes[:, :, :, lo - 1 : hi - 1], in0=e4[:, :, :, lo:hi], in1=c4[:, :, :, lo:hi], op=ALU.mult
-                )
+            nc.vector.tensor_tensor(
+                out=tt_planes[c // 2][:, :, first : first + CW].rearrange("p k (j t) -> p j t k", t=PACK),
+                in0=e4[:, :, :, 1:4],
+                in1=c4[:, :, :, 1:4],
+                op=ALU.mult,
+            )
+            nc.vector.tensor_tensor(
+                out=tt_pairs[c // 2][:, :, first : first + CW, :].rearrange("p q (j t) u -> p j t q u", t=PACK),
+                in0=e4[:, :, :, 4:K].rearrange("p j t (q u) -> p j t q u", u=2),
+                in1=c4[:, :, :, 4:K].rearrange("p j t (q u) -> p j t q u", u=2),
+                op=ALU.mult,
+            )
+
+        def new_products(pair, slot):
+            tl = big.tile([P, NPRIM * 2 * CW], F32, name="tt%d" % pair, tag=slot, align_bytes=64)
+            tt_planes[pair] = tl[:, : 3 * 2 * CW].rearrange("p (k n) -> p k n", k=3)
+            tt_pairs[pair] = tl[:, 3 * 2 * CW :].rearrange("p (q n u) -> p q n u", q=2, u=2)
+
+        def products(pair, lo, hi):
+            if hi <= 3:
+                return tt_planes[pair][:, lo:hi, :]
+            q, u = divmod(lo - 3, 2)
+            return tt_pairs[pair][:, q, :, u : u + hi - lo].rearrange("p n u -> p u n")
 
         def quant_prim(k, src):
             nc.vector.quantize_mx(out=pc[:, k, :].bitcast(FP8X4), scales=ps[:, k, :], in_=src)
@@ -221,7 +239,7 @@ def tile_dartslayer_kernel(tc, x, alphas, coeffs, out):
         nc.scalar.activation(out=lnx[:], in_=xg[:], func=ACT.Ln)
         p_ln = prim_tile("p_ln", "s5")
         nc.scalar.activation(out=p_ln[:], in_=xg[:], func=ACT.Ln)
-        tt[0] = big.tile([P, NPRIM, 2 * CW], F32, name="tt0", tag="t0", align_bytes=64)
+        new_products(0, "t0")
         times_coeffs(0)
         rt = k8.tile([P, NCH, CW], F32, name="rt", tag="s4", align_bytes=64)
         for c in range(NCH):
@@ -230,7 +248,7 @@ def tile_dartslayer_kernel(tc, x, alphas, coeffs, out):
             for q in range(PACK):
                 nc.tensor.transpose(rb[c][:, q, :], rt[:, c, q * P : (q + 1) * P], ident[:])
         times_coeffs(1)
-        tt[1] = big.tile([P, NPRIM, 2 * CW], F32, name="tt1", tag="e0", align_bytes=64)
+        new_products(1, "e0")
         times_coeffs(2)
         rr = k8.tile([P, NCH, CW], F32, name="rr", tag="s6", align_bytes=64)
         for c in range(NCH):
@@ -259,7 +277,7 @@ def tile_dartslayer_kernel(tc, x, alphas, coeffs, out):
                 inv = rr[:, 2 * pair : 2 * pair + 2, :].rearrange("p c n -> p (c n)")
                 nc.vector.tensor_tensor(
                     out=wq[:, at : at + hi - lo, 2 * pair * CW : 2 * (pair + 1) * CW],
-                    in0=tt[pair][:, lo:hi, :],
+                    in0=products(pair, lo, hi),
                     in1=inv.unsqueeze(1).to_broadcast([P, hi - lo, 2 * CW]),
                     op=ALU.mult,
                 )
@@ -285,9 +303,9 @@ def tile_dartslayer_kernel(tc, x, alphas, coeffs, out):
                     stop=(k == LAST),
                 )
 
-        def quant_rows(k, src, half):
-            words = slice(half * NB * P // 2, (half + 1) * NB * P // 2)
-            cols = slice(half * XW // 2, (half + 1) * XW // 2)
+        def quant_rows(k, src, blocks):
+            words = slice(blocks[0] * P, (blocks[-1] + 1) * P)
+            cols = slice(blocks[0] * P * PACK, (blocks[-1] + 1) * P * PACK)
             nc.vector.quantize_mx(out=pc[:, k, words].bitcast(FP8X4), scales=ps[:, k, words], in_=src[:, cols])
 
         p_exp = prim_tile("p_exp", "s4")
@@ -310,7 +328,7 @@ def tile_dartslayer_kernel(tc, x, alphas, coeffs, out):
         ROWS = (range(4), range(4, NB))
 
         def rows_of(k, src, half):
-            quant_rows(k, src, half)
+            quant_rows(k, src, ROWS[half])
             multiply(k, ROWS[half])
 
         wq_c = scaled_tile(2, "s2")
@@ -336,14 +354,19 @@ def tile_dartslayer_kernel(tc, x, alphas, coeffs, out):
         scale_planes(wq_d, 1, 6, 7, (1,))
         rows_of(1, p_sq, 1)
         quant_planes(wq_d, 1, 6, 7)
-        rows_of(6, p_sin, 0)
-        quant_rows(5, p_rec, 1)
-        quant_rows(6, p_sin, 1)
-        for pair in ((4, 5), (6, 7)):
+        for pair in (range(0, 2), range(2, 4)):
+            quant_rows(6, p_sin, pair)
+            multiply(6, pair)
+        quant_rows(5, p_rec, ROWS[1])
+        quant_rows(6, p_sin, ROWS[1])
+        for pair in (range(4, 6), range(6, 8)):
             multiply(5, pair)
             multiply(6, pair)
         ost = big.tile([P, NB, J], F32, name="ost", tag="l", align_bytes=64)
-        for b in range(0, NB, 2):
-            nc.scalar.copy(out=ost[:, b, :], in_=acc[b][:])
-            nc.vector.tensor_copy(out=ost[:, b + 1, :], in_=acc[b + 1][:])
-            nc.sync.dma_start(out=out_view[:, b : b + 2, :], in_=ost[:, b : b + 2, :])
+        for b in range(NB):
+            if b in (2, 4, 6):
+                nc.vector.tensor_copy(out=ost[:, b, :], in_=acc[b][:])
+            else:
+                nc.scalar.copy(out=ost[:, b, :], in_=acc[b][:])
+            if b % 2 == 1:
+                nc.sync.dma_start(out=out_view[:, b - 1 : b + 1, :], in_=ost[:, b - 1 : b + 1, :])

@@ -73,8 +73,9 @@ def tile_dartslayer_kernel(tc, x, alphas, coeffs, out):
         PIECES = ((0, QJ, HALF, JC), (0, HALF, JC), WHOLE, WHOLE)
         for c in range(NCH):
             a_sb[c] = load_chunk(a_view, c, "a%d" % c, PIECES[c])
-        x_sb = k8.tile([P, XW], BF16, name="x_sb", tag="s4", align_bytes=64)
-        nc.sync.dma_start(out=x_sb[:], in_=x_view)
+            if c == 1:
+                x_sb = k8.tile([P, XW], BF16, name="x_sb", tag="s4", align_bytes=64)
+                nc.sync.dma_start(out=x_sb[:], in_=x_view)
 
         ident = const.tile([P, P], F32, name="ident")
         make_identity(nc, ident[:])
@@ -123,10 +124,13 @@ def tile_dartslayer_kernel(tc, x, alphas, coeffs, out):
             flat = e_part(c, j0, nj).rearrange("p j t k -> p (j t k)")
             nc.scalar.activation(out=flat, in_=flat, func=ACT.Exp)
 
-        def sub_exp_vector(c, m3, j0, nj, off):
+        def sub_vector(c, m3, j0, nj, off):
             nc.vector.tensor_tensor(
                 out=e_part(c, j0, nj), in0=a_by_j(c, j0, nj), in1=spread(m3, off, nj), op=ALU.subtract
             )
+
+        def sub_exp_vector(c, m3, j0, nj, off):
+            sub_vector(c, m3, j0, nj, off)
             exp_sbuf(c, j0, nj)
 
         def sub_exp_tensor(c, m3, j0, off):
@@ -183,6 +187,34 @@ def tile_dartslayer_kernel(tc, x, alphas, coeffs, out):
         def prim_tile(label, slot):
             return k8.tile([P, XW], BF16, name=label, tag=slot, align_bytes=64)
 
+        MIXED = [(unit, half) for unit in range(3) for half in range(2)]
+
+        def sub_mixed(bank, unit, half):
+            first = half * 4
+            nc.tensor.matmul(
+                out=bank[:].rearrange("p (j t) k -> p j t k", t=PACK),
+                lhsT=ident_bf[:],
+                rhs=columns(a_sb[3], WHOLE, unit * QJ, QJ).rearrange("p t (j k) -> p j t k", k=K)[:, :, :, first : first + 4],
+                start=True,
+                stop=False,
+            )
+            for k in range(4):
+                nc.tensor.matmul(
+                    out=bank[:, :, k],
+                    lhsT=neg_max[:, unit, :],
+                    rhs=ident[:],
+                    is_transpose=True,
+                    start=False,
+                    stop=(k == 3),
+                )
+
+        def exp_mixed(bank, unit, half):
+            nc.scalar.activation(
+                out=e_part(3, unit * QJ, QJ)[:, :, :, half * 4 : half * 4 + 4].rearrange("p j t k -> p (j t) k"),
+                in_=bank[:],
+                func=ACT.Exp,
+            )
+
         new_e(0)
         todo = [(0, start, end - start) for start, end in zip(PIECES[0], PIECES[0][1:])] + [(1, 0, HALF)]
         m2 = tree2(tree1(*todo[0]), todo[0][2])
@@ -196,17 +228,10 @@ def tile_dartslayer_kernel(tc, x, alphas, coeffs, out):
         c_sb[0] = load_chunk(c_view, 0, "c0", WHOLE)
         m1_1b = tree1(1, HALF, HALF)
         m3_1a = tree3(m2_1a, HALF)
-        for q in range(3):
-            sub_exp_tensor(1, m3_1a, q * TJ, q * TJ)
         m2_1b = tree2(m1_1b, HALF)
-        sub_exp_vector(1, m3_1a, 3 * TJ, TJ, 3 * TJ)
+        sub_exp_vector(1, m3_1a, 0, QJ, 0)
         m3_1b = tree3(m2_1b, HALF)
-        new_e(1)
-        m1_2 = tree1(2, 0, JC)
-        sub_exp_vector(1, m3_1b, HALF, QJ, 0)
-        m2_2 = tree2(m1_2, JC)
-        sub_exp_vector(1, m3_1b, HALF + QJ, QJ, QJ)
-        c_sb[1] = load_chunk(c_view, 1, "c1", WHOLE)
+        sub_exp_vector(1, m3_1a, QJ, QJ, QJ)
 
         xw = x_sb[:].bitcast(F32).rearrange("p (b r u) -> p b u r", b=NB, u=2)
         xgw = xg[:].bitcast(F32).rearrange("p (b r u) -> p b r u", b=NB, u=2)
@@ -216,23 +241,45 @@ def tile_dartslayer_kernel(tc, x, alphas, coeffs, out):
                 for u in range(2):
                     nc.tensor.transpose(xt[:, b2, u, :], xw[:, 2 * h + b2, u, :], ident[:])
             nc.scalar.copy(out=xgw[:, 2 * h : 2 * h + 2, :, :], in_=xt[:].rearrange("p b u r -> p b r u"))
+        banks = [pst.tile([P, P, 4], F32, name="mix%d" % i, tag="t4") for i in range(2)]
+        sum_chunk(0)
+
+        new_e(1)
+        m1_2 = tree1(2, 0, JC)
+        sub_exp_vector(1, m3_1b, HALF, QJ, 0)
+        m2_2 = tree2(m1_2, JC)
+        sub_exp_vector(1, m3_1b, HALF + QJ, QJ, QJ)
+        c_sb[1] = load_chunk(c_view, 1, "c1", WHOLE)
+        sum_chunk(1)
         n_u = big.tile([P, XW], U32, name="n_u", tag="n", align_bytes=64)
         nc.scalar.activation(out=n_u[:], in_=xg[:], func=ACT.Copy, scale=0.5 / math.pi)
-        sum_chunk(0)
-        sum_chunk(1)
 
         m3_2 = tree3(m2_2, JC)
         m1_3 = tree1(3, 0, JC)
-        sub_exp_vector(2, m3_2, 0, HALF, 0)
+        sub_vector(2, m3_2, 0, QJ, 0)
         m2_3 = tree2(m1_3, JC)
+        sub_vector(2, m3_2, QJ, QJ, QJ)
+        m3_3 = tree3(m2_3, JC)
+        turned = psa.tile([P, 3, P], BF16, name="turned", tag="acc")
+        for u in range(3):
+            nc.tensor.transpose(
+                turned[:, u, :], m3_3[:, u * QJ : (u + 1) * QJ, :].rearrange("p j t -> p (j t)"), ident_bf[:]
+            )
+        neg_max = const.tile([P, 3, P], F32, name="neg_max")
+        nc.scalar.activation(out=neg_max[:], in_=turned[:], func=ACT.Copy, scale=-1.0)
+        banks += [psa.tile([P, P, 4], F32, name="mix%d" % i, tag="acc") for i in range(2, len(MIXED))]
+        for bank, place in zip(banks, MIXED):
+            sub_mixed(bank, *place)
+        exp_sbuf(2, 0, QJ)
+        exp_sbuf(2, QJ, QJ)
         sub_exp_vector(2, m3_2, HALF, HALF, HALF)
         c_sb[2] = load_chunk(c_view, 2, "c2", WHOLE)
-        sum_chunk(2)
-        m3_3 = tree3(m2_3, JC)
-        sub_exp_vector(3, m3_3, 0, HALF, 0)
-        sub_exp_vector(3, m3_3, HALF, QJ, HALF)
-        sub_exp_vector(3, m3_3, HALF + QJ, QJ, HALF + QJ)
+        sub_vector(3, m3_3, 3 * QJ, QJ, 3 * QJ)
+        for bank, place in zip(banks, MIXED):
+            exp_mixed(bank, *place)
+        exp_sbuf(3, 3 * QJ, QJ)
         c_sb[3] = load_chunk(c_view, 3, "c3", WHOLE)
+        sum_chunk(2)
         sum_chunk(3)
 
         lnx = big.tile([P, XW], F32, name="lnx", tag="l", align_bytes=64)
@@ -253,11 +300,11 @@ def tile_dartslayer_kernel(tc, x, alphas, coeffs, out):
         rr = k8.tile([P, NCH, CW], F32, name="rr", tag="s6", align_bytes=64)
         for c in range(NCH):
             nc.scalar.activation(out=rr[:, c, :], in_=rb[c][:].rearrange("p q n -> p (q n)"), func=ACT.Exp, scale=-1.0)
-        times_coeffs(3)
         y = n_u[:].bitcast(F32)
         nc.vector.scalar_tensor_tensor(
             out=y, in0=n_u[:].bitcast(I32), scalar=-2.0 * math.pi, in1=xg[:], op0=ALU.mult, op1=ALU.add
         )
+        times_coeffs(3)
         pc = big.tile([P, NPRIM, NB * P], U32, name="pc", tag="e1", align_bytes=64)
         quant_prim(0, xg[:])
         quant_prim(4, p_ln[:])

import math
from contextlib import ExitStack

import concourse.mybir as mybir
from concourse.masks import make_identity

F32 = mybir.dt.float32
BF16 = mybir.dt.bfloat16
I32 = mybir.dt.int32
U32 = mybir.dt.uint32
U8 = mybir.dt.uint8
FP8X4 = mybir.dt.float8_e4m3fn_x4
ALU = mybir.AluOpType
ACT = mybir.ActivationFunctionType

P = 128
B, I, J, K = 1024, 512, 512, 8
NB = B // P
PACK = 4
JC = 128
NCH = J // JC
NPRIM = K - 1
XW = NB * P * PACK
CW = JC * PACK
TJ = 16
HALF = JC // 2

FLOPS = 2 * B * I * J * NPRIM


def tile_dartslayer_kernel(tc, x, alphas, coeffs, out):
    nc = tc.nc
    with ExitStack() as ctx:
        const = ctx.enter_context(tc.tile_pool(name="const", bufs=1))
        big = ctx.enter_context(tc.tile_pool(name="big", bufs=1))
        k8 = ctx.enter_context(tc.tile_pool(name="k8", bufs=1))
        keep = ctx.enter_context(tc.tile_pool(name="keep", bufs=1))
        mt = ctx.enter_context(tc.tile_pool(name="mt", bufs=2))
        pst = ctx.enter_context(tc.psum_pool(name="pst", bufs=4))
        psa = ctx.enter_context(tc.psum_pool(name="psa", bufs=4))
        ctx.enter_context(tc.manual_schedule())

        a_view = alphas.rearrange("(p t) j k -> p t (j k)", t=PACK)
        c_view = coeffs.rearrange("(p t) j k -> p t (j k)", t=PACK)
        x_view = x.rearrange("(r b) i -> r (b i)", b=NB)
        out_view = out.rearrange("(r b) j -> r b j", b=NB)

        def piece(tl, start, end):
            return tl[:, start * PACK * K : end * PACK * K].rearrange("p (t w) -> p t w", t=PACK)

        def load_chunk(view, c, label, bounds):
            tl = k8.tile([P, JC * PACK * K], BF16, name=label, tag="s%d" % c, align_bytes=64)
            for start, end in zip(bounds, bounds[1:]):
                nc.sync.dma_start(
                    out=piece(tl, start, end), in_=view[:, :, (c * JC + start) * K : (c * JC + end) * K]
                )
            return tl

        def columns(tl, bounds, j0, nj):
            start, end = [(a, b) for a, b in zip(bounds, bounds[1:]) if a <= j0 and j0 + nj <= b][0]
            return piece(tl, start, end)[:, :, (j0 - start) * K : (j0 - start + nj) * K]

        a_sb = [None] * NCH
        c_sb = [None] * NCH
        e_pair = [None] * (NCH // 2)
        st = [None] * NCH
        rb = [None] * NCH
        tt_planes = [None] * (NCH // 2)
        tt_pairs = [None] * (NCH // 2)

        QJ = JC // 4
        WHOLE = (0, JC)
        PIECES = ((0, QJ, HALF, JC), (0, HALF, JC), WHOLE, WHOLE)
        for c in range(NCH):
            a_sb[c] = load_chunk(a_view, c, "a%d" % c, PIECES[c])
            if c == 1:
                x_sb = k8.tile([P, XW], BF16, name="x_sb", tag="s4", align_bytes=64)
                nc.sync.dma_start(out=x_sb[:], in_=x_view)

        ident = const.tile([P, P], F32, name="ident")
        make_identity(nc, ident[:])
        ident_bf = const.tile([P, P], BF16, name="ident_bf")
        nc.vector.tensor_copy(out=ident_bf[:], in_=ident[:])
        neg_bf = const.tile([P, P], BF16, name="neg_bf")
        nc.vector.tensor_scalar(out=neg_bf[:], in0=ident[:], scalar1=-1.0, scalar2=None, op0=ALU.mult)
        warm = const.tile([P, 1], F32, name="warm")
        nc.scalar.activation(out=warm[:], in_=ident[:, 0:1], func=ACT.Exp)

        xg = keep.tile([P, XW], BF16, name="xg", align_bytes=64)
        ps = keep.tile([P, NPRIM, NB * P], U8, name="ps", align_bytes=64)
        wc = keep.tile([P, NPRIM, J], U32, name="wc", align_bytes=64)
        ws = keep.tile([P, NPRIM, J], U8, name="ws", align_bytes=64)

        def new_e(pair):
            e_pair[pair] = big.tile([P, 2 * JC, PACK, K], F32, name="e%d" % pair, tag="e%d" % pair, align_bytes=64)

        def e_part(c, j0, nj):
            first = (c % 2) * JC + j0
            return e_pair[c // 2][:, first : first + nj]

        def a_by_j(c, j0, nj):
            return columns(a_sb[c], PIECES[c], j0, nj).rearrange("p t (j k) -> p j t k", k=K)

        def tree1(c, j0, nj):
            a6 = columns(a_sb[c], PIECES[c], j0, nj).rearrange("p t (j g f) -> p g j t f", g=2, f=4)
            m1 = mt.tile([P, nj, PACK, 4], BF16, name="m1")
            nc.vector.tensor_tensor(out=m1[:], in0=a6[:, 0], in1=a6[:, 1], op=ALU.max)
            return m1

        def tree2(m1, nj):
            m2 = mt.tile([P, nj, PACK, 2], BF16, name="m2")
            nc.vector.tensor_tensor(out=m2[:], in0=m1[:, :, :, 0:2], in1=m1[:, :, :, 2:4], op=ALU.max)
            return m2

        def tree3(m2, nj):
            m3 = mt.tile([P, nj, PACK], BF16, name="m3", bufs=4)
            nc.vector.tensor_tensor(out=m3[:], in0=m2[:, :, :, 0], in1=m2[:, :, :, 1], op=ALU.max)
            return m3

        def spread(m3, off, nj):
            return m3[:, off : off + nj, :].unsqueeze(3).to_broadcast([P, nj, PACK, K])

        def exp_sbuf(c, j0, nj):
            flat = e_part(c, j0, nj).rearrange("p j t k -> p (j t k)")
            nc.scalar.activation(out=flat, in_=flat, func=ACT.Exp)

        def sub_vector(c, m3, j0, nj, off):
            nc.vector.tensor_tensor(
                out=e_part(c, j0, nj), in0=a_by_j(c, j0, nj), in1=spread(m3, off, nj), op=ALU.subtract
            )

        def sub_exp_vector(c, m3, j0, nj, off):
            sub_vector(c, m3, j0, nj, off)
            exp_sbuf(c, j0, nj)

        def sub_exp_tensor(c, m3, j0, off):
            dps = psa.tile([P, TJ, PACK, K], F32, name="dps", tag="acc")
            nc.tensor.matmul(out=dps[:], lhsT=ident_bf[:], rhs=a_by_j(c, j0, TJ), start=True, stop=False)
            nc.tensor.matmul(out=dps[:], lhsT=neg_bf[:], rhs=spread(m3, off, TJ), start=False, stop=True)
            nc.scalar.activation(out=e_part(c, j0, TJ), in_=dps[:], func=ACT.Exp)

        def sum_chunk(c):
            e2 = e_part(c, 0, JC).rearrange("p j t k -> p (j t) k")
            st[c] = pst.tile([P, PACK, P], F32, name="st", tag="t4")
            for q in range(PACK):
                for k in range(K):
                    nc.tensor.matmul(
                        out=st[c][:, q, :],
                        lhsT=e2[:, q * P : (q + 1) * P, k],
                        rhs=ident[:],
                        is_transpose=True,
                        start=(k == 0),
                        stop=(k == K - 1),
                    )

        def times_coeffs(c):
            first = (c % 2) * CW
            e4 = e_part(c, 0, JC)
            c4 = columns(c_sb[c], WHOLE, 0, JC).rearrange("p t (j k) -> p j t k", k=K)
            nc.vector.tensor_tensor(
                out=tt_planes[c // 2][:, :, first : first + CW].rearrange("p k (j t) -> p j t k", t=PACK),
                in0=e4[:, :, :, 1:4],
                in1=c4[:, :, :, 1:4],
                op=ALU.mult,
            )
            nc.vector.tensor_tensor(
                out=tt_pairs[c // 2][:, :, first : first + CW, :].rearrange("p q (j t) u -> p j t q u", t=PACK),
                in0=e4[:, :, :, 4:K].rearrange("p j t (q u) -> p j t q u", u=2),
                in1=c4[:, :, :, 4:K].rearrange("p j t (q u) -> p j t q u", u=2),
                op=ALU.mult,
            )

        def new_products(pair, slot):
            tl = big.tile([P, NPRIM * 2 * CW], F32, name="tt%d" % pair, tag=slot, align_bytes=64)
            tt_planes[pair] = tl[:, : 3 * 2 * CW].rearrange("p (k n) -> p k n", k=3)
            tt_pairs[pair] = tl[:, 3 * 2 * CW :].rearrange("p (q n u) -> p q n u", q=2, u=2)

        def products(pair, lo, hi):
            if hi <= 3:
                return tt_planes[pair][:, lo:hi, :]
            q, u = divmod(lo - 3, 2)
            return tt_pairs[pair][:, q, :, u : u + hi - lo].rearrange("p n u -> p u n")

        def quant_prim(k, src):
            nc.vector.quantize_mx(out=pc[:, k, :].bitcast(FP8X4), scales=ps[:, k, :], in_=src)

        def prim_tile(label, slot):
            return k8.tile([P, XW], BF16, name=label, tag=slot, align_bytes=64)

        MIXED = [(unit, half) for unit in range(3) for half in range(2)]

        def sub_mixed(bank, unit, half):
            first = half * 4
            nc.tensor.matmul(
                out=bank[:].rearrange("p (j t) k -> p j t k", t=PACK),
                lhsT=ident_bf[:],
                rhs=columns(a_sb[3], WHOLE, unit * QJ, QJ).rearrange("p t (j k) -> p j t k", k=K)[:, :, :, first : first + 4],
                start=True,
                stop=False,
            )
            for k in range(4):
                nc.tensor.matmul(
                    out=bank[:, :, k],
                    lhsT=neg_max[:, unit, :],
                    rhs=ident[:],
                    is_transpose=True,
                    start=False,
                    stop=(k == 3),
                )

        def exp_mixed(bank, unit, half):
            nc.scalar.activation(
                out=e_part(3, unit * QJ, QJ)[:, :, :, half * 4 : half * 4 + 4].rearrange("p j t k -> p (j t) k"),
                in_=bank[:],
                func=ACT.Exp,
            )

        new_e(0)
        todo = [(0, start, end - start) for start, end in zip(PIECES[0], PIECES[0][1:])] + [(1, 0, HALF)]
        m2 = tree2(tree1(*todo[0]), todo[0][2])
        for this, following in zip(todo, todo[1:]):
            m1_next = tree1(*following)
            m3 = tree3(m2, this[2])
            for q in range(this[2] // TJ):
                sub_exp_tensor(0, m3, this[1] + q * TJ, q * TJ)
            m2 = tree2(m1_next, following[2])
        m2_1a = m2
        c_sb[0] = load_chunk(c_view, 0, "c0", WHOLE)
        m1_1b = tree1(1, HALF, HALF)
        m3_1a = tree3(m2_1a, HALF)
        m2_1b = tree2(m1_1b, HALF)
        sub_exp_vector(1, m3_1a, 0, QJ, 0)
        m3_1b = tree3(m2_1b, HALF)
        sub_exp_vector(1, m3_1a, QJ, QJ, QJ)

        xw = x_sb[:].bitcast(F32).rearrange("p (b r u) -> p b u r", b=NB, u=2)
        xgw = xg[:].bitcast(F32).rearrange("p (b r u) -> p b r u", b=NB, u=2)
        for h in range(NB // 2):
            xt = psa.tile([P, 2, 2, P], F32, name="xt", tag="acc")
            for b2 in range(2):
                for u in range(2):
                    nc.tensor.transpose(xt[:, b2, u, :], xw[:, 2 * h + b2, u, :], ident[:])
            nc.scalar.copy(out=xgw[:, 2 * h : 2 * h + 2, :, :], in_=xt[:].rearrange("p b u r -> p b r u"))
        banks = [pst.tile([P, P, 4], F32, name="mix%d" % i, tag="t4") for i in range(2)]
        sum_chunk(0)

        new_e(1)
        m1_2 = tree1(2, 0, JC)
        sub_exp_vector(1, m3_1b, HALF, QJ, 0)
        m2_2 = tree2(m1_2, JC)
        sub_exp_vector(1, m3_1b, HALF + QJ, QJ, QJ)
        c_sb[1] = load_chunk(c_view, 1, "c1", WHOLE)
        sum_chunk(1)
        n_u = big.tile([P, XW], U32, name="n_u", tag="n", align_bytes=64)
        nc.scalar.activation(out=n_u[:], in_=xg[:], func=ACT.Copy, scale=0.5 / math.pi)

        m3_2 = tree3(m2_2, JC)
        m1_3 = tree1(3, 0, JC)
        sub_vector(2, m3_2, 0, QJ, 0)
        m2_3 = tree2(m1_3, JC)
        sub_vector(2, m3_2, QJ, QJ, QJ)
        m3_3 = tree3(m2_3, JC)
        turned = psa.tile([P, 3, P], BF16, name="turned", tag="acc")
        for u in range(3):
            nc.tensor.transpose(
                turned[:, u, :], m3_3[:, u * QJ : (u + 1) * QJ, :].rearrange("p j t -> p (j t)"), ident_bf[:]
            )
        neg_max = const.tile([P, 3, P], F32, name="neg_max")
        nc.scalar.activation(out=neg_max[:], in_=turned[:], func=ACT.Copy, scale=-1.0)
        banks += [psa.tile([P, P, 4], F32, name="mix%d" % i, tag="acc") for i in range(2, len(MIXED))]
        for bank, place in zip(banks, MIXED):
            sub_mixed(bank, *place)
        exp_sbuf(2, 0, QJ)
        exp_sbuf(2, QJ, QJ)
        sub_exp_vector(2, m3_2, HALF, HALF, HALF)
        c_sb[2] = load_chunk(c_view, 2, "c2", WHOLE)
        sub_vector(3, m3_3, 3 * QJ, QJ, 3 * QJ)
        for bank, place in zip(banks, MIXED):
            exp_mixed(bank, *place)
        exp_sbuf(3, 3 * QJ, QJ)
        c_sb[3] = load_chunk(c_view, 3, "c3", WHOLE)
        sum_chunk(2)
        sum_chunk(3)

        lnx = big.tile([P, XW], F32, name="lnx", tag="l", align_bytes=64)
        nc.scalar.activation(out=lnx[:], in_=xg[:], func=ACT.Ln)
        p_ln = prim_tile("p_ln", "s5")
        nc.scalar.activation(out=p_ln[:], in_=xg[:], func=ACT.Ln)
        new_products(0, "t0")
        times_coeffs(0)
        rt = k8.tile([P, NCH, CW], F32, name="rt", tag="s4", align_bytes=64)
        for c in range(NCH):
            nc.scalar.activation(out=rt[:, c, :], in_=st[c][:].rearrange("p q n -> p (q n)"), func=ACT.Ln)
            rb[c] = psa.tile([P, PACK, P], F32, name="rb", tag="acc")
            for q in range(PACK):
                nc.tensor.transpose(rb[c][:, q, :], rt[:, c, q * P : (q + 1) * P], ident[:])
        times_coeffs(1)
        new_products(1, "e0")
        times_coeffs(2)
        rr = k8.tile([P, NCH, CW], F32, name="rr", tag="s6", align_bytes=64)
        for c in range(NCH):
            nc.scalar.activation(out=rr[:, c, :], in_=rb[c][:].rearrange("p q n -> p (q n)"), func=ACT.Exp, scale=-1.0)
        y = n_u[:].bitcast(F32)
        nc.vector.scalar_tensor_tensor(
            out=y, in0=n_u[:].bitcast(I32), scalar=-2.0 * math.pi, in1=xg[:], op0=ALU.mult, op1=ALU.add
        )
        times_coeffs(3)
        pc = big.tile([P, NPRIM, NB * P], U32, name="pc", tag="e1", align_bytes=64)
        quant_prim(0, xg[:])
        quant_prim(4, p_ln[:])

        acc = []
        for b in range(NB):
            if b < 4:
                acc.append(psa.tile([P, J], F32, name="acc%d" % b, tag="acc"))
            else:
                acc.append(pst.tile([P, J], F32, name="acc%d" % b, tag="t4"))

        def scaled_tile(planes, slot):
            return k8.tile([P, planes, NCH * CW], BF16, name="wq", tag=slot, align_bytes=64)

        def scale_planes(wq, at, lo, hi, pairs=range(NCH // 2)):
            for pair in pairs:
                inv = rr[:, 2 * pair : 2 * pair + 2, :].rearrange("p c n -> p (c n)")
                nc.vector.tensor_tensor(
                    out=wq[:, at : at + hi - lo, 2 * pair * CW : 2 * (pair + 1) * CW],
                    in0=products(pair, lo, hi),
                    in1=inv.unsqueeze(1).to_broadcast([P, hi - lo, 2 * CW]),
                    op=ALU.mult,
                )

        def quant_planes(wq, at, lo, hi):
            nc.vector.quantize_mx(
                out=wc[:, lo:hi, :].rearrange("p k n -> p (k n)").bitcast(FP8X4),
                scales=ws[:, lo:hi, :].rearrange("p k n -> p (k n)"),
                in_=wq[:, at : at + hi - lo, :].rearrange("p k n -> p (k n)"),
            )

        FIRST, LAST = 4, 6

        def multiply(k, blocks=range(NB)):
            for b in blocks:
                nc.tensor.matmul_mx(
                    out=acc[b][:],
                    lhsT=pc[:, k, b * P : (b + 1) * P].bitcast(FP8X4),
                    lhsT_scale=ps[:, k, b * P : (b + 1) * P],
                    rhs=wc[:, k, :].bitcast(FP8X4),
                    rhs_scale=ws[:, k, :],
                    start=(k == FIRST),
                    stop=(k == LAST),
                )

        def quant_rows(k, src, blocks):
            words = slice(blocks[0] * P, (blocks[-1] + 1) * P)
            cols = slice(blocks[0] * P * PACK, (blocks[-1] + 1) * P * PACK)
            nc.vector.quantize_mx(out=pc[:, k, words].bitcast(FP8X4), scales=ps[:, k, words], in_=src[:, cols])

        p_exp = prim_tile("p_exp", "s4")
        nc.scalar.activation(out=p_exp[:], in_=xg[:], func=ACT.Exp)
        p_cube = prim_tile("p_cube", "s5")
        nc.scalar.activation(out=p_cube[:], in_=lnx[:], func=ACT.Exp, scale=3.0)
        wq_a = scaled_tile(2, "s0")
        scale_planes(wq_a, 0, 3, 5)
        wq_b = scaled_tile(2, "s1")
        scale_planes(wq_b, 0, 0, 1)
        quant_planes(wq_a, 0, 3, 5)
        multiply(4)
        quant_prim(3, p_exp[:])
        multiply(3)
        p_rec = prim_tile("p_rec", "s3")
        nc.scalar.activation(out=p_rec[:], in_=lnx[:], func=ACT.Exp, scale=-1.0)
        p_sq = prim_tile("p_sq", "s0")
        nc.scalar.activation(out=p_sq[:], in_=xg[:], func=ACT.Square)
        p_sin = prim_tile("p_sin", "s1")
        ROWS = (range(4), range(4, NB))

        def rows_of(k, src, half):
            quant_rows(k, src, ROWS[half])
            multiply(k, ROWS[half])

        wq_c = scaled_tile(2, "s2")
        scale_planes(wq_c, 1, 2, 3)
        quant_planes(wq_b, 0, 0, 1)
        multiply(0)
        for i in range(2):
            cols = slice(i * XW // 2, (i + 1) * XW // 2)
            nc.scalar.activation(out=p_sin[:, cols], in_=y[:, cols], func=ACT.Sin)
        scale_planes(wq_c, 0, 1, 2, (0,))
        quant_planes(wq_c, 1, 2, 3)
        scale_planes(wq_c, 0, 1, 2, (1,))
        rows_of(2, p_cube, 0)
        wq_d = scaled_tile(2, "s4")
        scale_planes(wq_d, 0, 5, 6, (0,))
        quant_planes(wq_c, 0, 1, 2)
        rows_of(2, p_cube, 1)
        scale_planes(wq_d, 0, 5, 6, (1,))
        rows_of(1, p_sq, 0)
        quant_planes(wq_d, 0, 5, 6)
        scale_planes(wq_d, 1, 6, 7, (0,))
        rows_of(5, p_rec, 0)
        scale_planes(wq_d, 1, 6, 7, (1,))
        rows_of(1, p_sq, 1)
        quant_planes(wq_d, 1, 6, 7)
        for pair in (range(0, 2), range(2, 4)):
            quant_rows(6, p_sin, pair)
            multiply(6, pair)
        quant_rows(5, p_rec, ROWS[1])
        quant_rows(6, p_sin, ROWS[1])
        for pair in (range(4, 6), range(6, 8)):
            multiply(5, pair)
            multiply(6, pair)
        ost = big.tile([P, NB, J], F32, name="ost", tag="l", align_bytes=64)
        for b in range(NB):
            if b in (2, 4, 6):
                nc.vector.tensor_copy(out=ost[:, b, :], in_=acc[b][:])
            else:
                nc.scalar.copy(out=ost[:, b, :], in_=acc[b][:])
            if b % 2 == 1:
                nc.sync.dma_start(out=out_view[:, b - 1 : b + 1, :], in_=ost[:, b - 1 : b + 1, :])
